import numpy as np
import ml_dtypes


def mxq(x, axis, fmt="e4m3"):
    dtype, down = {"e4m3": (ml_dtypes.float8_e4m3fn, 7), "e5m2": (ml_dtypes.float8_e5m2, 14)}[fmt]
    v = np.moveaxis(np.asarray(x, np.float32).astype(ml_dtypes.bfloat16).astype(np.float64), axis, -1)
    blocks = v.reshape(v.shape[:-1] + (-1, 32))
    amax = np.abs(blocks).max(-1, keepdims=True)
    byte = np.maximum(np.where(amax > 0, np.frexp(amax)[1] - 1 + 127, 0) - down, 1)
    scale = np.exp2(byte - 127.0)
    codes = (blocks / scale).astype(np.float32).astype(dtype).astype(np.float64)
    return np.moveaxis((codes * scale).reshape(v.shape), -1, axis)


WIDE = False


def mx_kscale(k):
    if not WIDE:
        return np.ones(k)
    levels = np.array([10, -10, 5, -5, 0])
    a = np.random.permutation(np.resize(levels, k // 512 * 4)).reshape(k // 512, 4)
    idx = np.arange(k)
    return np.exp2(a[idx // 512, idx % 128 // 32])


BF16 = ml_dtypes.bfloat16


def bf(x):
    return np.asarray(x, np.float32).astype(BF16)


def f64(x):
    return np.asarray(x).astype(np.float64)


B, D, L, H = 128, 1024, 128, 1024


def setup_inputs():
    s, t = mx_kscale(D), mx_kscale(H)
    return {
        "x": bf((np.random.random((B, D)) < 0.5) * s),
        "eps": bf(np.random.standard_normal((B, L))),
        "We1": bf(np.random.standard_normal((D, H)) * 1.4 / np.sqrt(D) / s[:, None] * t),
        "be1": bf(np.random.standard_normal(H) * 0.3 * t),
        "Wmu": bf(np.random.standard_normal((H, L)) * 1.4 / np.sqrt(H) / t[:, None]),
        "bmu": bf(np.random.standard_normal(L) * 0.3),
        "Wls": bf(np.random.standard_normal((H, L)) * 0.7 / np.sqrt(H) / t[:, None]),
        "bls": bf(np.random.standard_normal(L) * 0.2),
    }


def reference(x, eps, We1, be1, Wmu, bmu, Wls, bls):
    h = np.maximum((mxq(f64(x), 1, "e4m3") @ mxq(f64(We1), 0, "e4m3")) + f64(be1), 0.0)
    hq = mxq(h, 1, "e4m3")
    mu = (hq @ mxq(f64(Wmu), 0, "e4m3")) + f64(bmu)
    logsigma = (hq @ mxq(f64(Wls), 0, "e4m3")) + f64(bls)
    z = mu + np.exp(logsigma) * f64(eps)
    kl = 0.5 * np.sum(np.exp(2.0 * logsigma) + mu * mu - 2.0 * logsigma - 1.0, axis=-1)
    return z, kl

@@ -1,0 +1,247 @@
+from contextlib import ExitStack
+
+import concourse.mybir as mybir
+from concourse.masks import make_identity
+
+F32 = mybir.dt.float32
+BF16 = mybir.dt.bfloat16
+U32 = mybir.dt.uint32
+U8 = mybir.dt.uint8
+FP8X4 = mybir.dt.float8_e4m3fn_x4
+ACT = mybir.ActivationFunctionType
+ALU = mybir.AluOpType
+
+P = 128
+PACK = 4
+K_PASS = P * PACK
+
+BATCH = 128
+D_IN = 1024
+HIDDEN = 1024
+LATENT = 128
+D_PASSES = D_IN // K_PASS
+H_PASSES = HIDDEN // K_PASS
+HEADS = 2
+
+FLOPS = 2 * BATCH * D_IN * HIDDEN + HEADS * 2 * BATCH * HIDDEN * LATENT
+
+
+def quantise(nc, values, codes, scales):
+    nc.vector.quantize_mx(out=codes.bitcast(FP8X4), scales=scales, in_=values)
+
+
+def tile_vae_pa_s_kernel(tc, x, eps, We1, be1, Wmu, bmu, Wls, bls, out_0, out_1):
+    nc = tc.nc
+    with ExitStack() as ctx:
+        keep = ctx.enter_context(tc.tile_pool(name="keep", bufs=1))
+        chunks = ctx.enter_context(tc.tile_pool(name="chunks", bufs=D_PASSES * H_PASSES))
+        hidden = ctx.enter_context(tc.tile_pool(name="hidden", bufs=H_PASSES))
+        psum = ctx.enter_context(tc.psum_pool(name="psum", bufs=1))
+
+        x_sb = keep.tile([P, D_IN], BF16)
+        nc.sync.dma_start(out=x_sb[:], in_=x)
+
+        w_raw = {}
+        for c in range(H_PASSES):
+            for g in range(D_PASSES):
+                raw = chunks.tile([P, PACK, K_PASS], BF16, name="w_raw")
+                nc.sync.dma_start(
+                    out=raw[:],
+                    in_=We1[g * K_PASS : (g + 1) * K_PASS, c * K_PASS : (c + 1) * K_PASS].rearrange(
+                        "(p j) w -> p j w", j=PACK
+                    ),
+                )
+                w_raw[(c, g)] = raw
+
+        head_raw = keep.tile([P, HEADS, H_PASSES, PACK, LATENT], BF16)
+        for head, weights in enumerate((Wmu, Wls)):
+            nc.sync.dma_start(
+                out=head_raw[:, head].rearrange("p g t l -> p g (t l)"),
+                in_=weights.rearrange("(g p t) l -> p g (t l)", g=H_PASSES, t=PACK),
+            )
+
+        be1_bf = keep.tile([P, H_PASSES, PACK], BF16)
+        nc.scalar.dma_start(out=be1_bf[:], in_=be1.rearrange("(c p t) -> p c t", c=H_PASSES, t=PACK))
+        head_bias_row = keep.tile([P, HEADS * LATENT], BF16)
+        nc.vector.memset(head_bias_row[:], 0.0)
+        for head, bias in enumerate((bmu, bls)):
+            nc.scalar.dma_start(
+                out=head_bias_row[0:1, head * LATENT : (head + 1) * LATENT],
+                in_=bias.rearrange("(o l) -> o l", o=1),
+            )
+        eps_sb = keep.tile([P, LATENT], BF16)
+        nc.scalar.dma_start(out=eps_sb[:], in_=eps)
+
+        ident = keep.tile([P, P], F32)
+        make_identity(nc, ident[:])
+        ones = keep.tile([P, P], BF16)
+        nc.vector.memset(ones[:], 1.0)
+        zeros = keep.tile([P, P], F32)
+        nc.vector.memset(zeros[:], 0.0)
+
+        table_in = keep.tile([P, 1], F32)
+        nc.vector.memset(table_in[:], 0.0)
+        table_out = keep.tile([P, 1], F32)
+        nc.scalar.activation(out=table_out[:], in_=table_in[:], func=ACT.Exp)
+
+        be1_f32 = keep.tile([P, H_PASSES, PACK], F32)
+        nc.vector.tensor_copy(out=be1_f32[:], in_=be1_bf[:])
+
+        head_bias_ps = psum.tile([P, HEADS, LATENT], F32)
+        nc.tensor.matmul(
+            out=head_bias_ps[:].rearrange("p h l -> p (h l)"),
+            lhsT=ones[:],
+            rhs=head_bias_row[:],
+            start=True,
+            stop=True,
+        )
+        head_bias = keep.tile([P, HEADS, LATENT], F32)
+        nc.scalar.copy(out=head_bias[:], in_=head_bias_ps[:])
+
+        x_words = x_sb[:].bitcast(F32).rearrange("b (g p u) -> b g u p", g=D_PASSES, u=2)
+        x_t = psum.tile([P, D_PASSES, 2, BATCH], F32)
+        for g in range(D_PASSES):
+            for u in range(2):
+                nc.tensor.transpose(out=x_t[:, g, u, :], in_=x_words[:, g, u, :], identity=ident[:])
+        x_grouped = keep.tile([P, D_PASSES * BATCH * PACK], BF16, align_bytes=64)
+        nc.vector.tensor_copy(
+            out=x_grouped[:].bitcast(F32).rearrange("p (g b u) -> p g b u", g=D_PASSES, u=2),
+            in_=x_t[:].rearrange("p g u b -> p g b u"),
+        )
+        x_codes = keep.tile([P, D_PASSES, BATCH], U32, align_bytes=64)
+        x_scales = keep.tile([P, D_PASSES, BATCH], U8, align_bytes=64)
+        quantise(
+            nc,
+            x_grouped[:],
+            x_codes[:].rearrange("p g b -> p (g b)"),
+            x_scales[:].rearrange("p g b -> p (g b)"),
+        )
+
+        w_codes = keep.tile([P, H_PASSES, D_PASSES, PACK, P], U32, align_bytes=64)
+        w_scales = keep.tile([P, H_PASSES, D_PASSES, PACK, P], U8, align_bytes=64)
+        h_codes = keep.tile([P, H_PASSES, BATCH], U32, align_bytes=64)
+        h_scales = keep.tile([P, H_PASSES, BATCH], U8, align_bytes=64)
+        head_grouped = keep.tile([P, HEADS, H_PASSES, LATENT, PACK], BF16, align_bytes=64)
+        head_codes = keep.tile([P, HEADS, H_PASSES, LATENT], U32, align_bytes=64)
+        head_scales = keep.tile([P, HEADS, H_PASSES, LATENT], U8, align_bytes=64)
+
+        for c in range(H_PASSES):
+            acc = []
+            for t in range(PACK):
+                acc.append(psum.tile([P, BATCH], F32, name="acc%d" % t))
+            for g in range(D_PASSES):
+                by_tile = w_raw[(c, g)][:].rearrange("p j (q a e) -> p a q j e", a=2, e=2)
+                grouped = chunks.tile([P, 2, 2, P, PACK], BF16, name="w_grouped", align_bytes=64)
+                nc.vector.tensor_copy(out=grouped[:, 0].rearrange("p e q j -> p q j e"), in_=by_tile[:, 0])
+                nc.scalar.copy(out=grouped[:, 1].rearrange("p e q j -> p q j e"), in_=by_tile[:, 1])
+                for a in range(2):
+                    quantise(
+                        nc,
+                        grouped[:, a].rearrange("p e q j -> p (e q j)"),
+                        w_codes[:, c, g, 2 * a : 2 * a + 2, :].rearrange("p e q -> p (e q)"),
+                        w_scales[:, c, g, 2 * a : 2 * a + 2, :].rearrange("p e q -> p (e q)"),
+                    )
+                for t in range(PACK):
+                    nc.tensor.matmul_mx(
+                        out=acc[t][:],
+                        lhsT=w_codes[:, c, g, t, :].bitcast(FP8X4),
+                        lhsT_scale=w_scales[:, c, g, t, :],
+                        rhs=x_codes[:, g, :].bitcast(FP8X4),
+                        rhs_scale=x_scales[:, g, :],
+                        start=(g == 0),
+                        stop=(g == D_PASSES - 1),
+                    )
+
+            h_plain = hidden.tile([P, PACK, BATCH], BF16)
+            for t in range(PACK):
+                nc.scalar.activation(
+                    out=h_plain[:, t, :], in_=acc[t][:], func=ACT.Relu, bias=be1_f32[:, c, t : t + 1]
+                )
+            h_grouped = hidden.tile([P, BATCH, PACK], BF16, align_bytes=64)
+            nc.vector.tensor_copy(
+                out=h_grouped[:].rearrange("p (n i) t -> p n t i", i=4),
+                in_=h_plain[:].rearrange("p t (n i) -> p n t i", i=4),
+            )
+            quantise(nc, h_grouped[:].rearrange("p b t -> p (b t)"), h_codes[:, c, :], h_scales[:, c, :])
+
+        for head in range(HEADS):
+            nc.vector.tensor_copy(
+                out=head_grouped[:, head, 0].rearrange("p (n i) t -> p n t i", i=4),
+                in_=head_raw[:, head, 0].rearrange("p t (n i) -> p n t i", i=4),
+            )
+            nc.scalar.copy(
+                out=head_grouped[:, head, 1].rearrange("p (n i) t -> p n t i", i=4),
+                in_=head_raw[:, head, 1].rearrange("p t (n i) -> p n t i", i=4),
+            )
+            quantise(
+                nc,
+                head_grouped[:, head].rearrange("p g l t -> p (g l t)"),
+                head_codes[:, head].rearrange("p g l -> p (g l)"),
+                head_scales[:, head].rearrange("p g l -> p (g l)"),
+            )
+
+        mu_ps = psum.tile([P, LATENT], F32)
+        log_sigma_ps = psum.tile([P, LATENT], F32)
+        for head, sums in ((1, log_sigma_ps), (0, mu_ps)):
+            for c in range(H_PASSES):
+                nc.tensor.matmul_mx(
+                    out=sums[:],
+                    lhsT=h_codes[:, c, :].bitcast(FP8X4),
+                    lhsT_scale=h_scales[:, c, :],
+                    rhs=head_codes[:, head, c, :].bitcast(FP8X4),
+                    rhs_scale=head_scales[:, head, c, :],
+                    start=(c == 0),
+                    stop=(c == H_PASSES - 1),
+                )
+
+        log_sigma = keep.tile([P, LATENT], F32)
+        sum_log_sigma = keep.tile([P, 1], F32)
+        nc.vector.scalar_tensor_tensor(
+            out=log_sigma[:],
+            in0=log_sigma_ps[:],
+            scalar=1.0,
+            in1=head_bias[:, 1, :],
+            op0=ALU.mult,
+            op1=ALU.add,
+            accum_out=sum_log_sigma[:],
+        )
+        mu = keep.tile([P, LATENT], F32)
+        nc.vector.tensor_tensor(out=mu[:], in0=mu_ps[:], in1=head_bias[:, 0, :], op=ALU.add)
+
+        sigma_sq = keep.tile([P, LATENT], F32)
+        sum_sigma_sq = keep.tile([P, 1], F32)
+        nc.scalar.activation(
+            out=sigma_sq[:], in_=log_sigma[:], func=ACT.Exp, scale=2.0, accum_out=sum_sigma_sq[:]
+        )
+        sigma = keep.tile([P, LATENT], F32)
+        nc.scalar.activation(out=sigma[:], in_=log_sigma[:], func=ACT.Exp)
+        mu_sq = keep.tile([P, LATENT], F32)
+        sum_mu_sq = keep.tile([P, 1], F32)
+        nc.scalar.activation(out=mu_sq[:], in_=mu[:], func=ACT.Square, accum_out=sum_mu_sq[:])
+
+        noise = keep.tile([P, LATENT], F32)
+        nc.vector.tensor_tensor(out=noise[:], in0=sigma[:], in1=eps_sb[:], op=ALU.mult)
+        z = keep.tile([P, LATENT], F32)
+        nc.vector.tensor_tensor(out=z[:], in0=noise[:], in1=mu[:], op=ALU.add)
+        nc.sync.dma_start(out=out_0, in_=z[:])
+
+        sum_squares = keep.tile([P, 1], F32)
+        nc.vector.tensor_tensor(out=sum_squares[:], in0=sum_sigma_sq[:], in1=sum_mu_sq[:], op=ALU.add)
+        kl = keep.tile([P, 1], F32)
+        nc.vector.scalar_tensor_tensor(
+            out=kl[:], in0=sum_squares[:], scalar=0.5, in1=sum_log_sigma[:], op0=ALU.mult, op1=ALU.subtract
+        )
+        kl_spread = keep.tile([P, P], F32)
+        nc.vector.tensor_scalar(
+            out=kl_spread[:],
+            in0=zeros[:],
+            scalar1=kl[:, 0:1],
+            scalar2=-0.5 * LATENT,
+            op0=ALU.add,
+            op1=ALU.add,
+        )
+        kl_t = psum.tile([P, P], F32, tag="x_t")
+        nc.tensor.transpose(out=kl_t[:], in_=kl_spread[:], identity=ident[:])
+        kl_rows = keep.tile([P, P], F32)
+        nc.vector.tensor_copy(out=kl_rows[:], in_=kl_t[:])
+        nc.sync.dma_start(out=out_1.rearrange("(o b) -> o b", o=1), in_=kl_rows[0:1, :])

@@ -19,75 +19,264 @@ BATCH = 128
 D_IN = 1024
 HIDDEN = 1024
 LATENT = 128
-D_PASSES = D_IN // K_PASS
-H_PASSES = HIDDEN // K_PASS
-HEADS = 2
+G = D_IN // K_PASS
+C = HIDDEN // K_PASS
+U = 2
+E = 2
+W_UNIT = E * P
+MU, LS = 0, 1
 
-FLOPS = 2 * BATCH * D_IN * HIDDEN + HEADS * 2 * BATCH * HIDDEN * LATENT
+V_WORDS = 80
+V_WORDS_LS = 88
 
-
-def quantise(nc, values, codes, scales):
-    nc.vector.quantize_mx(out=codes.bitcast(FP8X4), scales=scales, in_=values)
+FLOPS = 2 * BATCH * D_IN * HIDDEN + 2 * 2 * BATCH * HIDDEN * LATENT
 
 
 def tile_vae_pa_s_kernel(tc, x, eps, We1, be1, Wmu, bmu, Wls, bls, out_0, out_1):
     nc = tc.nc
     with ExitStack() as ctx:
         keep = ctx.enter_context(tc.tile_pool(name="keep", bufs=1))
-        chunks = ctx.enter_context(tc.tile_pool(name="chunks", bufs=D_PASSES * H_PASSES))
-        hidden = ctx.enter_context(tc.tile_pool(name="hidden", bufs=H_PASSES))
         psum = ctx.enter_context(tc.psum_pool(name="psum", bufs=1))
+        ctx.enter_context(tc.manual_schedule())
 
-        x_sb = keep.tile([P, D_IN], BF16)
-        nc.sync.dma_start(out=x_sb[:], in_=x)
+        be1_rows = keep.tile([P, P * E], BF16)
+        nc.vector.memset(be1_rows[:], 0.0)
+
+        def load_w(name, g, c0, width):
+            raw = keep.tile([P, PACK, width], BF16, name=name)
+            nc.sync.dma_start(
+                out=raw[:],
+                in_=We1[g * K_PASS : (g + 1) * K_PASS, c0 : c0 + width].rearrange("(p j) w -> p j w", j=PACK),
+            )
+            return raw
+
+        def load_head(name, weights):
+            raw = keep.tile([P, C, U, E * LATENT], BF16, name=name)
+            nc.sync.dma_start(out=raw[:], in_=weights.rearrange("(c u p e) l -> p c u (e l)", c=C, u=U, e=E))
+            return raw
 
         w_raw = {}
-        for c in range(H_PASSES):
-            for g in range(D_PASSES):
-                raw = chunks.tile([P, PACK, K_PASS], BF16, name="w_raw")
-                nc.sync.dma_start(
-                    out=raw[:],
-                    in_=We1[g * K_PASS : (g + 1) * K_PASS, c * K_PASS : (c + 1) * K_PASS].rearrange(
-                        "(p j) w -> p j w", j=PACK
-                    ),
-                )
-                w_raw[(c, g)] = raw
+        w_raw[(0, 0, 0)] = load_w("w000", 0, 0, W_UNIT)[:]
+        nc.sync.dma_start(out=be1_rows[0 : C * U, :], in_=be1.rearrange("(r w) -> r w", r=C * U))
+        w_raw[(0, 0, 1)] = load_w("w001", 0, W_UNIT, W_UNIT)[:]
+        x_sb = keep.tile([P, D_IN], BF16)
+        nc.sync.dma_start(out=x_sb[:], in_=x)
+        w01 = load_w("w01", 1, 0, K_PASS)
+        ls_raw = load_head("ls_raw", Wls)
+        w10 = load_w("w10", 0, K_PASS, K_PASS)
+        w11 = load_w("w11", 1, K_PASS, K_PASS)
+        mu_raw = load_head("mu_raw", Wmu)
+        for u in range(U):
+            cols = slice(u * W_UNIT, (u + 1) * W_UNIT)
+            w_raw[(0, 1, u)] = w01[:, :, cols]
+            w_raw[(1, 0, u)] = w10[:, :, cols]
+            w_raw[(1, 1, u)] = w11[:, :, cols]
 
-        head_raw = keep.tile([P, HEADS, H_PASSES, PACK, LATENT], BF16)
-        for head, weights in enumerate((Wmu, Wls)):
-            nc.sync.dma_start(
-                out=head_raw[:, head].rearrange("p g t l -> p g (t l)"),
-                in_=weights.rearrange("(g p t) l -> p g (t l)", g=H_PASSES, t=PACK),
-            )
-
-        be1_bf = keep.tile([P, H_PASSES, PACK], BF16)
-        nc.scalar.dma_start(out=be1_bf[:], in_=be1.rearrange("(c p t) -> p c t", c=H_PASSES, t=PACK))
-        head_bias_row = keep.tile([P, HEADS * LATENT], BF16)
+        ident = keep.tile([P, P], F32)
+        make_identity(nc, ident[:])
+        head_bias_row = keep.tile([P, 2 * LATENT], BF16)
         nc.vector.memset(head_bias_row[:], 0.0)
-        for head, bias in enumerate((bmu, bls)):
-            nc.scalar.dma_start(
+        ones = keep.tile([P, P], BF16)
+        nc.vector.memset(ones[:], 1.0)
+        kl_cols = keep.tile([P, 32], F32, align_bytes=64)
+        nc.vector.memset(kl_cols[:], 0.0)
+        for head, bias in ((MU, bmu), (LS, bls)):
+            nc.sync.dma_start(
                 out=head_bias_row[0:1, head * LATENT : (head + 1) * LATENT],
                 in_=bias.rearrange("(o l) -> o l", o=1),
             )
         eps_sb = keep.tile([P, LATENT], BF16)
-        nc.scalar.dma_start(out=eps_sb[:], in_=eps)
-
-        ident = keep.tile([P, P], F32)
-        make_identity(nc, ident[:])
-        ones = keep.tile([P, P], BF16)
-        nc.vector.memset(ones[:], 1.0)
-        zeros = keep.tile([P, P], F32)
-        nc.vector.memset(zeros[:], 0.0)
+        nc.sync.dma_start(out=eps_sb[:], in_=eps)
 
         table_in = keep.tile([P, 1], F32)
         nc.vector.memset(table_in[:], 0.0)
         table_out = keep.tile([P, 1], F32)
         nc.scalar.activation(out=table_out[:], in_=table_in[:], func=ACT.Exp)
 
-        be1_f32 = keep.tile([P, H_PASSES, PACK], F32)
-        nc.vector.tensor_copy(out=be1_f32[:], in_=be1_bf[:])
+        def bank(name, index, shape):
+            return psum.tile(shape, F32, name=name, tag="bank%d" % index)
 
-        head_bias_ps = psum.tile([P, HEADS, LATENT], F32)
+        x_t = bank("x_t", 7, [P, G, 2, BATCH])
+        be1_t = bank("be1_t", 5, [P, P])
+        be1_words = keep.tile([P, C * U], F32)
+        be1_sb = be1_words[:].bitcast(BF16).rearrange("p (c u e) -> p c u e", c=C, u=U)
+        acc = {}
+
+        x_grouped = keep.tile([P, G * BATCH * PACK], BF16, align_bytes=64)
+        x_codes = keep.tile([P, G, BATCH], U32, align_bytes=64)
+        x_scales = keep.tile([P, G, BATCH], U8, align_bytes=64)
+        w_grouped, w_codes, w_scales = {}, {}, {}
+        h_plain, h_grouped, h_codes, h_scales = {}, {}, {}, {}
+
+        def x_transposes():
+            words = x_sb[:].bitcast(F32).rearrange("b (g p u) -> b g u p", g=G, u=2)
+            for g in range(G):
+                for u in range(2):
+                    nc.tensor.transpose(out=x_t[:, g, u, :], in_=words[:, g, u, :], identity=ident[:])
+
+        def x_copy():
+            nc.scalar.copy(
+                out=x_grouped[:].bitcast(F32).rearrange("p (g b u) -> p g b u", g=G, u=2),
+                in_=x_t[:].rearrange("p g u b -> p g b u"),
+            )
+
+        def x_quantise():
+            nc.vector.quantize_mx(
+                out=x_codes[:].rearrange("p g b -> p (g b)").bitcast(FP8X4),
+                scales=x_scales[:].rearrange("p g b -> p (g b)"),
+                in_=x_grouped[:],
+            )
+
+        def w_copy(unit):
+            tag = "%d%d%d" % unit
+            grouped = keep.tile([P, E, P, PACK], BF16, name="w_grouped" + tag, align_bytes=64)
+            w_grouped[unit] = grouped
+            src = w_raw[unit].rearrange("p j (q e) -> p q j e", e=E)
+            dst = grouped[:].rearrange("p e q j -> p q j e")
+            nc.vector.tensor_copy(out=dst[:, :V_WORDS], in_=src[:, :V_WORDS])
+            nc.scalar.copy(out=dst[:, V_WORDS:], in_=src[:, V_WORDS:])
+
+        def w_quantise(unit):
+            tag = "%d%d%d" % unit
+            w_codes[unit] = keep.tile([P, E, P], U32, name="w_codes" + tag, align_bytes=64)
+            w_scales[unit] = keep.tile([P, E, P], U8, name="w_scales" + tag, align_bytes=64)
+            nc.vector.quantize_mx(
+                out=w_codes[unit][:].rearrange("p e q -> p (e q)").bitcast(FP8X4),
+                scales=w_scales[unit][:].rearrange("p e q -> p (e q)"),
+                in_=w_grouped[unit][:].rearrange("p e q j -> p (e q j)"),
+            )
+
+        def w_matmul(unit):
+            c, g, u = unit
+            for e in range(E):
+                t = E * u + e
+                if g == 0:
+                    acc[(c, t)] = bank("acc%d%d" % (c, t), 4 * c + t, [P, BATCH])
+                nc.tensor.matmul_mx(
+                    out=acc[(c, t)][:],
+                    lhsT=w_codes[unit][:, e, :].bitcast(FP8X4),
+                    lhsT_scale=w_scales[unit][:, e, :],
+                    rhs=x_codes[:, g, :].bitcast(FP8X4),
+                    rhs_scale=x_scales[:, g, :],
+                    start=(g == 0),
+                    stop=(g == G - 1),
+                )
+
+        def relu_scalar(c, u, e):
+            nc.scalar.activation(
+                out=h_plain[(c, u)][:, e, :],
+                in_=acc[(c, E * u + e)][:],
+                func=ACT.Relu,
+                bias=be1_sb[:, c, u, e : e + 1],
+            )
+
+        def relu_vector(c, u, e):
+            nc.vector.tensor_scalar(
+                out=h_plain[(c, u)][:, e, :],
+                in0=acc[(c, E * u + e)][:],
+                scalar1=be1_sb[:, c, u, e : e + 1],
+                scalar2=0.0,
+                op0=ALU.add,
+                op1=ALU.max,
+            )
+
+        def h_copy(c, u):
+            nc.vector.tensor_copy(
+                out=h_grouped[c][:, :, E * u : E * u + E], in_=h_plain[(c, u)][:].rearrange("p e b -> p b e")
+            )
+
+        def h_quantise(c):
+            nc.vector.quantize_mx(
+                out=h_codes[c][:].bitcast(FP8X4),
+                scales=h_scales[c][:],
+                in_=h_grouped[c][:].rearrange("p b t -> p (b t)"),
+            )
+
+        for c in range(C):
+            h_grouped[c] = keep.tile([P, BATCH, PACK], BF16, name="h_grouped%d" % c, align_bytes=64)
+            h_codes[c] = keep.tile([P, BATCH], U32, name="h_codes%d" % c, align_bytes=64)
+            h_scales[c] = keep.tile([P, BATCH], U8, name="h_scales%d" % c, align_bytes=64)
+            for u in range(U):
+                h_plain[(c, u)] = keep.tile([P, E, BATCH], BF16, name="h_plain%d%d" % (c, u))
+
+        head_grouped, head_codes, head_scales = {}, {}, {}
+        for head in (LS, MU):
+            head_grouped[head] = keep.tile([P, C, LATENT, PACK], BF16, name="head_grouped%d" % head, align_bytes=64)
+            head_codes[head] = keep.tile([P, C, LATENT], U32, name="head_codes%d" % head, align_bytes=64)
+            head_scales[head] = keep.tile([P, C, LATENT], U8, name="head_scales%d" % head, align_bytes=64)
+        head_raw = {LS: ls_raw, MU: mu_raw}
+
+        def head_copy(copy, head, c, lo, hi):
+            src = head_raw[head][:, c].rearrange("p u (e l) -> p (u e) l", e=E)[:, :, lo:hi]
+            dst = head_grouped[head][:, c, lo:hi, :]
+            copy(
+                out=dst.rearrange("p (n i) t -> p n t i", i=4),
+                in_=src.rearrange("p t (n i) -> p n t i", i=4),
+            )
+
+        def head_quantise(head):
+            nc.vector.quantize_mx(
+                out=head_codes[head][:].rearrange("p c l -> p (c l)").bitcast(FP8X4),
+                scales=head_scales[head][:].rearrange("p c l -> p (c l)"),
+                in_=head_grouped[head][:].rearrange("p c l t -> p (c l t)"),
+            )
+
+        sums = {}
+
+        def head_matmul(head, c):
+            if c == 0:
+                sums[head] = bank("sums%d" % head, head, [P, LATENT])
+            nc.tensor.matmul_mx(
+                out=sums[head][:],
+                lhsT=h_codes[c][:].bitcast(FP8X4),
+                lhsT_scale=h_scales[c][:],
+                rhs=head_codes[head][:, c, :].bitcast(FP8X4),
+                rhs_scale=head_scales[head][:, c, :],
+                start=(c == 0),
+                stop=(c == C - 1),
+            )
+
+        w_copy((0, 0, 0))
+        w_copy((0, 0, 1))
+        w_quantise((0, 0, 0))
+        x_transposes()
+        nc.tensor.transpose(out=be1_t[:], in_=be1_rows[:].bitcast(F32), identity=ident[:])
+        x_copy()
+        nc.scalar.copy(out=be1_words[:], in_=be1_t[:, 0 : C * U])
+        w_copy((0, 1, 0))
+        w_quantise((0, 0, 1))
+        x_quantise()
+        w_matmul((0, 0, 0))
+        w_matmul((0, 0, 1))
+        w_copy((0, 1, 1))
+        w_quantise((0, 1, 0))
+        w_matmul((0, 1, 0))
+        head_copy(nc.vector.tensor_copy, LS, 0, 0, LATENT)
+        head_copy(nc.scalar.copy, LS, 1, 0, LATENT)
+        w_quantise((0, 1, 1))
+        w_matmul((0, 1, 1))
+        relu_scalar(0, 0, 0)
+        relu_scalar(0, 0, 1)
+        w_copy((1, 0, 0))
+        head_quantise(LS)
+        relu_scalar(0, 1, 0)
+        relu_scalar(0, 1, 1)
+        w_copy((1, 0, 1))
+        w_quantise((1, 0, 0))
+        w_matmul((1, 0, 0))
+        h_copy(0, 0)
+        h_copy(0, 1)
+        w_copy((1, 1, 0))
+        w_quantise((1, 0, 1))
+        w_matmul((1, 0, 1))
+        h_quantise(0)
+        head_matmul(LS, 0)
+        w_copy((1, 1, 1))
+        w_quantise((1, 1, 0))
+        w_matmul((1, 1, 0))
+        w_quantise((1, 1, 1))
+        w_matmul((1, 1, 1))
+        head_bias_ps = bank("head_bias_ps", 2, [P, 2, LATENT])
         nc.tensor.matmul(
             out=head_bias_ps[:].rearrange("p h l -> p (h l)"),
             lhsT=ones[:],
@@ -95,153 +284,61 @@ def tile_vae_pa_s_kernel(tc, x, eps, We1, be1, Wmu, bmu, Wls, bls, out_0, out_1)
             start=True,
             stop=True,
         )
-        head_bias = keep.tile([P, HEADS, LATENT], F32)
+        head_copy(nc.scalar.copy, MU, 0, 0, LATENT // 2)
+        relu_scalar(1, 0, 0)
+        relu_vector(1, 0, 1)
+        head_copy(nc.scalar.copy, MU, 0, LATENT // 2, LATENT)
+        h_copy(1, 0)
+        relu_scalar(1, 1, 0)
+        relu_vector(1, 1, 1)
+        head_bias = keep.tile([P, 2, LATENT], F32)
         nc.scalar.copy(out=head_bias[:], in_=head_bias_ps[:])
-
-        x_words = x_sb[:].bitcast(F32).rearrange("b (g p u) -> b g u p", g=D_PASSES, u=2)
-        x_t = psum.tile([P, D_PASSES, 2, BATCH], F32)
-        for g in range(D_PASSES):
-            for u in range(2):
-                nc.tensor.transpose(out=x_t[:, g, u, :], in_=x_words[:, g, u, :], identity=ident[:])
-        x_grouped = keep.tile([P, D_PASSES * BATCH * PACK], BF16, align_bytes=64)
-        nc.vector.tensor_copy(
-            out=x_grouped[:].bitcast(F32).rearrange("p (g b u) -> p g b u", g=D_PASSES, u=2),
-            in_=x_t[:].rearrange("p g u b -> p g b u"),
-        )
-        x_codes = keep.tile([P, D_PASSES, BATCH], U32, align_bytes=64)
-        x_scales = keep.tile([P, D_PASSES, BATCH], U8, align_bytes=64)
-        quantise(
-            nc,
-            x_grouped[:],
-            x_codes[:].rearrange("p g b -> p (g b)"),
-            x_scales[:].rearrange("p g b -> p (g b)"),
-        )
-
-        w_codes = keep.tile([P, H_PASSES, D_PASSES, PACK, P], U32, align_bytes=64)
-        w_scales = keep.tile([P, H_PASSES, D_PASSES, PACK, P], U8, align_bytes=64)
-        h_codes = keep.tile([P, H_PASSES, BATCH], U32, align_bytes=64)
-        h_scales = keep.tile([P, H_PASSES, BATCH], U8, align_bytes=64)
-        head_grouped = keep.tile([P, HEADS, H_PASSES, LATENT, PACK], BF16, align_bytes=64)
-        head_codes = keep.tile([P, HEADS, H_PASSES, LATENT], U32, align_bytes=64)
-        head_scales = keep.tile([P, HEADS, H_PASSES, LATENT], U8, align_bytes=64)
-
-        for c in range(H_PASSES):
-            acc = []
-            for t in range(PACK):
-                acc.append(psum.tile([P, BATCH], F32, name="acc%d" % t))
-            for g in range(D_PASSES):
-                by_tile = w_raw[(c, g)][:].rearrange("p j (q a e) -> p a q j e", a=2, e=2)
-                grouped = chunks.tile([P, 2, 2, P, PACK], BF16, name="w_grouped", align_bytes=64)
-                nc.vector.tensor_copy(out=grouped[:, 0].rearrange("p e q j -> p q j e"), in_=by_tile[:, 0])
-                nc.scalar.copy(out=grouped[:, 1].rearrange("p e q j -> p q j e"), in_=by_tile[:, 1])
-                for a in range(2):
-                    quantise(
-                        nc,
-                        grouped[:, a].rearrange("p e q j -> p (e q j)"),
-                        w_codes[:, c, g, 2 * a : 2 * a + 2, :].rearrange("p e q -> p (e q)"),
-                        w_scales[:, c, g, 2 * a : 2 * a + 2, :].rearrange("p e q -> p (e q)"),
-                    )
-                for t in range(PACK):
-                    nc.tensor.matmul_mx(
-                        out=acc[t][:],
-                        lhsT=w_codes[:, c, g, t, :].bitcast(FP8X4),
-                        lhsT_scale=w_scales[:, c, g, t, :],
-                        rhs=x_codes[:, g, :].bitcast(FP8X4),
-                        rhs_scale=x_scales[:, g, :],
-                        start=(g == 0),
-                        stop=(g == D_PASSES - 1),
-                    )
-
-            h_plain = hidden.tile([P, PACK, BATCH], BF16)
-            for t in range(PACK):
-                nc.scalar.activation(
-                    out=h_plain[:, t, :], in_=acc[t][:], func=ACT.Relu, bias=be1_f32[:, c, t : t + 1]
-                )
-            h_grouped = hidden.tile([P, BATCH, PACK], BF16, align_bytes=64)
-            nc.vector.tensor_copy(
-                out=h_grouped[:].rearrange("p (n i) t -> p n t i", i=4),
-                in_=h_plain[:].rearrange("p t (n i) -> p n t i", i=4),
-            )
-            quantise(nc, h_grouped[:].rearrange("p b t -> p (b t)"), h_codes[:, c, :], h_scales[:, c, :])
-
-        for head in range(HEADS):
-            nc.vector.tensor_copy(
-                out=head_grouped[:, head, 0].rearrange("p (n i) t -> p n t i", i=4),
-                in_=head_raw[:, head, 0].rearrange("p t (n i) -> p n t i", i=4),
-            )
-            nc.scalar.copy(
-                out=head_grouped[:, head, 1].rearrange("p (n i) t -> p n t i", i=4),
-                in_=head_raw[:, head, 1].rearrange("p t (n i) -> p n t i", i=4),
-            )
-            quantise(
-                nc,
-                head_grouped[:, head].rearrange("p g l t -> p (g l t)"),
-                head_codes[:, head].rearrange("p g l -> p (g l)"),
-                head_scales[:, head].rearrange("p g l -> p (g l)"),
-            )
-
-        mu_ps = psum.tile([P, LATENT], F32)
-        log_sigma_ps = psum.tile([P, LATENT], F32)
-        for head, sums in ((1, log_sigma_ps), (0, mu_ps)):
-            for c in range(H_PASSES):
-                nc.tensor.matmul_mx(
-                    out=sums[:],
-                    lhsT=h_codes[:, c, :].bitcast(FP8X4),
-                    lhsT_scale=h_scales[:, c, :],
-                    rhs=head_codes[:, head, c, :].bitcast(FP8X4),
-                    rhs_scale=head_scales[:, head, c, :],
-                    start=(c == 0),
-                    stop=(c == H_PASSES - 1),
-                )
+        head_copy(nc.scalar.copy, MU, 1, 0, LATENT)
+        h_copy(1, 1)
+        h_quantise(1)
+        head_matmul(LS, 1)
 
         log_sigma = keep.tile([P, LATENT], F32)
         sum_log_sigma = keep.tile([P, 1], F32)
         nc.vector.scalar_tensor_tensor(
             out=log_sigma[:],
-            in0=log_sigma_ps[:],
+            in0=sums[LS][:],
             scalar=1.0,
-            in1=head_bias[:, 1, :],
+            in1=head_bias[:, LS, :],
             op0=ALU.mult,
             op1=ALU.add,
             accum_out=sum_log_sigma[:],
         )
-        mu = keep.tile([P, LATENT], F32)
-        nc.vector.tensor_tensor(out=mu[:], in0=mu_ps[:], in1=head_bias[:, 0, :], op=ALU.add)
-
-        sigma_sq = keep.tile([P, LATENT], F32)
-        sum_sigma_sq = keep.tile([P, 1], F32)
-        nc.scalar.activation(
-            out=sigma_sq[:], in_=log_sigma[:], func=ACT.Exp, scale=2.0, accum_out=sum_sigma_sq[:]
-        )
         sigma = keep.tile([P, LATENT], F32)
         nc.scalar.activation(out=sigma[:], in_=log_sigma[:], func=ACT.Exp)
-        mu_sq = keep.tile([P, LATENT], F32)
-        sum_mu_sq = keep.tile([P, 1], F32)
-        nc.scalar.activation(out=mu_sq[:], in_=mu[:], func=ACT.Square, accum_out=sum_mu_sq[:])
-
+        head_quantise(MU)
+        head_matmul(MU, 0)
+        head_matmul(MU, 1)
         noise = keep.tile([P, LATENT], F32)
         nc.vector.tensor_tensor(out=noise[:], in0=sigma[:], in1=eps_sb[:], op=ALU.mult)
+        mu = keep.tile([P, LATENT], F32)
+        nc.vector.tensor_tensor(out=mu[:], in0=sums[MU][:], in1=head_bias[:, MU, :], op=ALU.add)
+        sigma_sq = keep.tile([P, LATENT], F32)
+        sum_sigma_sq = keep.tile([P, 1], F32)
+        nc.scalar.activation(out=sigma_sq[:], in_=log_sigma[:], func=ACT.Exp, scale=2.0, accum_out=sum_sigma_sq[:])
+        mu_sq = keep.tile([P, LATENT], F32)
+        half_mu_sq = keep.tile([P, 1], F32)
+        nc.scalar.activation(out=mu_sq[:], in_=mu[:], func=ACT.Square, scale=0.5**0.5, accum_out=half_mu_sq[:])
+        part = keep.tile([P, 1], F32)
+        half_sigma_sq = keep.tile([P, 1], F32)
+        nc.vector.tensor_scalar(
+            out=half_sigma_sq[:],
+            in0=sum_sigma_sq[:],
+            scalar1=0.5,
+            scalar2=-0.5 * LATENT,
+            op0=ALU.mult,
+            op1=ALU.add,
+        )
         z = keep.tile([P, LATENT], F32)
         nc.vector.tensor_tensor(out=z[:], in0=noise[:], in1=mu[:], op=ALU.add)
         nc.sync.dma_start(out=out_0, in_=z[:])
-
-        sum_squares = keep.tile([P, 1], F32)
-        nc.vector.tensor_tensor(out=sum_squares[:], in0=sum_sigma_sq[:], in1=sum_mu_sq[:], op=ALU.add)
-        kl = keep.tile([P, 1], F32)
-        nc.vector.scalar_tensor_tensor(
-            out=kl[:], in0=sum_squares[:], scalar=0.5, in1=sum_log_sigma[:], op0=ALU.mult, op1=ALU.subtract
-        )
-        kl_spread = keep.tile([P, P], F32)
-        nc.vector.tensor_scalar(
-            out=kl_spread[:],
-            in0=zeros[:],
-            scalar1=kl[:, 0:1],
-            scalar2=-0.5 * LATENT,
-            op0=ALU.add,
-            op1=ALU.add,
-        )
-        kl_t = psum.tile([P, P], F32, tag="x_t")
-        nc.tensor.transpose(out=kl_t[:], in_=kl_spread[:], identity=ident[:])
-        kl_rows = keep.tile([P, P], F32)
-        nc.vector.tensor_copy(out=kl_rows[:], in_=kl_t[:])
-        nc.sync.dma_start(out=out_1.rearrange("(o b) -> o b", o=1), in_=kl_rows[0:1, :])
+        nc.vector.tensor_tensor(out=part[:], in0=half_sigma_sq[:], in1=sum_log_sigma[:], op=ALU.subtract)
+        nc.vector.tensor_tensor(out=kl_cols[:, 0:1], in0=half_mu_sq[:], in1=part[:], op=ALU.add)
+        kl_rows = keep.tile([P, 32], F32, align_bytes=64)
+        nc.vector.transpose(kl_rows[:], kl_cols[:])
+        nc.scalar.dma_start(out=out_1.rearrange("(a b) -> a b", b=32), in_=kl_rows[0:P:32, :])

@@ -21,13 +21,12 @@ HIDDEN = 1024
 LATENT = 128
 G = D_IN // K_PASS
 C = HIDDEN // K_PASS
-U = 2
+A = 2
 E = 2
-W_UNIT = E * P
 MU, LS = 0, 1
 
-V_WORDS = 80
-V_WORDS_LS = 88
+V_WORDS = 68
+V_LATENT = 64
 
 FLOPS = 2 * BATCH * D_IN * HIDDEN + 2 * 2 * BATCH * HIDDEN * LATENT
 
@@ -39,55 +38,51 @@ def tile_vae_pa_s_kernel(tc, x, eps, We1, be1, Wmu, bmu, Wls, bls, out_0, out_1)
         psum = ctx.enter_context(tc.psum_pool(name="psum", bufs=1))
         ctx.enter_context(tc.manual_schedule())
 
-        be1_rows = keep.tile([P, P * E], BF16)
-        nc.vector.memset(be1_rows[:], 0.0)
-
-        def load_w(name, g, c0, width):
-            raw = keep.tile([P, PACK, width], BF16, name=name)
-            nc.sync.dma_start(
-                out=raw[:],
-                in_=We1[g * K_PASS : (g + 1) * K_PASS, c0 : c0 + width].rearrange("(p j) w -> p j w", j=PACK),
+        be1_sb = keep.tile([P, C, PACK], BF16)
+        nc.scalar.dma_start(out=be1_sb[:], in_=be1.rearrange("(c p t) -> p c t", c=C, t=PACK))
+        head_bias_row = keep.tile([P, 2 * LATENT], BF16)
+        nc.vector.memset(head_bias_row[:], 0.0)
+        for head, bias in ((MU, bmu), (LS, bls)):
+            nc.scalar.dma_start(
+                out=head_bias_row[0:1, head * LATENT : (head + 1) * LATENT],
+                in_=bias.rearrange("(o l) -> o l", o=1),
             )
-            return raw
 
-        def load_head(name, weights):
-            raw = keep.tile([P, C, U, E * LATENT], BF16, name=name)
-            nc.sync.dma_start(out=raw[:], in_=weights.rearrange("(c u p e) l -> p c u (e l)", c=C, u=U, e=E))
-            return raw
+        head_raw, w_raw = {}, {}
 
-        w_raw = {}
-        w_raw[(0, 0, 0)] = load_w("w000", 0, 0, W_UNIT)[:]
-        nc.sync.dma_start(out=be1_rows[0 : C * U, :], in_=be1.rearrange("(r w) -> r w", r=C * U))
-        w_raw[(0, 0, 1)] = load_w("w001", 0, W_UNIT, W_UNIT)[:]
+        def load_head(head, weights):
+            head_raw[head] = keep.tile([P, C, PACK, LATENT], BF16, name="head_raw%d" % head)
+            nc.sync.dma_start(
+                out=head_raw[head][:].rearrange("p c t l -> p c (t l)"),
+                in_=weights.rearrange("(c p t) l -> p c (t l)", c=C, t=PACK),
+            )
+
+        def load_w(c, g):
+            w_raw[(c, g)] = keep.tile([P, PACK, K_PASS], BF16, name="w_raw%d%d" % (c, g))
+            nc.sync.dma_start(
+                out=w_raw[(c, g)][:],
+                in_=We1[g * K_PASS : (g + 1) * K_PASS, c * K_PASS : (c + 1) * K_PASS].rearrange(
+                    "(p j) w -> p j w", j=PACK
+                ),
+            )
+
         x_sb = keep.tile([P, D_IN], BF16)
+        eps_sb = keep.tile([P, LATENT], BF16)
+        load_head(LS, Wls)
+        load_w(0, 0)
         nc.sync.dma_start(out=x_sb[:], in_=x)
-        w01 = load_w("w01", 1, 0, K_PASS)
-        ls_raw = load_head("ls_raw", Wls)
-        w10 = load_w("w10", 0, K_PASS, K_PASS)
-        w11 = load_w("w11", 1, K_PASS, K_PASS)
-        mu_raw = load_head("mu_raw", Wmu)
-        for u in range(U):
-            cols = slice(u * W_UNIT, (u + 1) * W_UNIT)
-            w_raw[(0, 1, u)] = w01[:, :, cols]
-            w_raw[(1, 0, u)] = w10[:, :, cols]
-            w_raw[(1, 1, u)] = w11[:, :, cols]
+        load_w(0, 1)
+        load_w(1, 0)
+        load_w(1, 1)
+        load_head(MU, Wmu)
+        nc.sync.dma_start(out=eps_sb[:], in_=eps)
 
         ident = keep.tile([P, P], F32)
         make_identity(nc, ident[:])
-        head_bias_row = keep.tile([P, 2 * LATENT], BF16)
-        nc.vector.memset(head_bias_row[:], 0.0)
         ones = keep.tile([P, P], BF16)
         nc.vector.memset(ones[:], 1.0)
         kl_cols = keep.tile([P, 32], F32, align_bytes=64)
         nc.vector.memset(kl_cols[:], 0.0)
-        for head, bias in ((MU, bmu), (LS, bls)):
-            nc.sync.dma_start(
-                out=head_bias_row[0:1, head * LATENT : (head + 1) * LATENT],
-                in_=bias.rearrange("(o l) -> o l", o=1),
-            )
-        eps_sb = keep.tile([P, LATENT], BF16)
-        nc.sync.dma_start(out=eps_sb[:], in_=eps)
-
         table_in = keep.tile([P, 1], F32)
         nc.vector.memset(table_in[:], 0.0)
         table_out = keep.tile([P, 1], F32)
@@ -97,16 +92,29 @@ def tile_vae_pa_s_kernel(tc, x, eps, We1, be1, Wmu, bmu, Wls, bls, out_0, out_1)
             return psum.tile(shape, F32, name=name, tag="bank%d" % index)
 
         x_t = bank("x_t", 7, [P, G, 2, BATCH])
-        be1_t = bank("be1_t", 5, [P, P])
-        be1_words = keep.tile([P, C * U], F32)
-        be1_sb = be1_words[:].bitcast(BF16).rearrange("p (c u e) -> p c u e", c=C, u=U)
         acc = {}
-
         x_grouped = keep.tile([P, G * BATCH * PACK], BF16, align_bytes=64)
         x_codes = keep.tile([P, G, BATCH], U32, align_bytes=64)
         x_scales = keep.tile([P, G, BATCH], U8, align_bytes=64)
         w_grouped, w_codes, w_scales = {}, {}, {}
         h_plain, h_grouped, h_codes, h_scales = {}, {}, {}, {}
+        head_grouped, head_codes, head_scales, sums = {}, {}, {}, {}
+        for c in range(C):
+            h_grouped[c] = keep.tile([P, BATCH, PACK], BF16, name="h_grouped%d" % c, align_bytes=64)
+            h_codes[c] = keep.tile([P, BATCH], U32, name="h_codes%d" % c, align_bytes=64)
+            h_scales[c] = keep.tile([P, BATCH], U8, name="h_scales%d" % c, align_bytes=64)
+            for a in range(A):
+                h_plain[(c, a)] = keep.tile([P, E, BATCH], BF16, name="h_plain%d%d" % (c, a))
+            for g in range(G):
+                for a in range(A):
+                    tag = "%d%d%d" % (c, g, a)
+                    w_grouped[(c, g, a)] = keep.tile([P, E, P, PACK], BF16, name="w_grouped" + tag, align_bytes=64)
+                    w_codes[(c, g, a)] = keep.tile([P, E, P], U32, name="w_codes" + tag, align_bytes=64)
+                    w_scales[(c, g, a)] = keep.tile([P, E, P], U8, name="w_scales" + tag, align_bytes=64)
+        for head in (LS, MU):
+            head_grouped[head] = keep.tile([P, C, LATENT, PACK], BF16, name="head_grouped%d" % head, align_bytes=64)
+            head_codes[head] = keep.tile([P, C, LATENT], U32, name="head_codes%d" % head, align_bytes=64)
+            head_scales[head] = keep.tile([P, C, LATENT], U8, name="head_scales%d" % head, align_bytes=64)
 
         def x_transposes():
             words = x_sb[:].bitcast(F32).rearrange("b (g p u) -> b g u p", g=G, u=2)
@@ -127,62 +135,55 @@ def tile_vae_pa_s_kernel(tc, x, eps, We1, be1, Wmu, bmu, Wls, bls, out_0, out_1)
                 in_=x_grouped[:],
             )
 
-        def w_copy(unit):
-            tag = "%d%d%d" % unit
-            grouped = keep.tile([P, E, P, PACK], BF16, name="w_grouped" + tag, align_bytes=64)
-            w_grouped[unit] = grouped
-            src = w_raw[unit].rearrange("p j (q e) -> p q j e", e=E)
-            dst = grouped[:].rearrange("p e q j -> p q j e")
+        def w_copy(c, g, a):
+            src = w_raw[(c, g)][:].rearrange("p j (q a e) -> p a q j e", a=A, e=E)[:, a]
+            dst = w_grouped[(c, g, a)][:].rearrange("p e q j -> p q j e")
             nc.vector.tensor_copy(out=dst[:, :V_WORDS], in_=src[:, :V_WORDS])
             nc.scalar.copy(out=dst[:, V_WORDS:], in_=src[:, V_WORDS:])
 
-        def w_quantise(unit):
-            tag = "%d%d%d" % unit
-            w_codes[unit] = keep.tile([P, E, P], U32, name="w_codes" + tag, align_bytes=64)
-            w_scales[unit] = keep.tile([P, E, P], U8, name="w_scales" + tag, align_bytes=64)
+        def w_quantise(c, g, a):
+            unit = (c, g, a)
             nc.vector.quantize_mx(
                 out=w_codes[unit][:].rearrange("p e q -> p (e q)").bitcast(FP8X4),
                 scales=w_scales[unit][:].rearrange("p e q -> p (e q)"),
                 in_=w_grouped[unit][:].rearrange("p e q j -> p (e q j)"),
             )
 
-        def w_matmul(unit):
-            c, g, u = unit
+        def w_matmul(c, g, a):
             for e in range(E):
-                t = E * u + e
+                t = E * a + e
                 if g == 0:
                     acc[(c, t)] = bank("acc%d%d" % (c, t), 4 * c + t, [P, BATCH])
                 nc.tensor.matmul_mx(
                     out=acc[(c, t)][:],
-                    lhsT=w_codes[unit][:, e, :].bitcast(FP8X4),
-                    lhsT_scale=w_scales[unit][:, e, :],
+                    lhsT=w_codes[(c, g, a)][:, e, :].bitcast(FP8X4),
+                    lhsT_scale=w_scales[(c, g, a)][:, e, :],
                     rhs=x_codes[:, g, :].bitcast(FP8X4),
                     rhs_scale=x_scales[:, g, :],
                     start=(g == 0),
                     stop=(g == G - 1),
                 )
 
-        def relu_scalar(c, u, e):
+        def relu_scalar(c, a, e):
+            t = E * a + e
             nc.scalar.activation(
-                out=h_plain[(c, u)][:, e, :],
-                in_=acc[(c, E * u + e)][:],
-                func=ACT.Relu,
-                bias=be1_sb[:, c, u, e : e + 1],
+                out=h_plain[(c, a)][:, e, :], in_=acc[(c, t)][:], func=ACT.Relu, bias=be1_sb[:, c, t : t + 1]
             )
 
-        def relu_vector(c, u, e):
+        def relu_vector(c, a, e):
+            t = E * a + e
             nc.vector.tensor_scalar(
-                out=h_plain[(c, u)][:, e, :],
-                in0=acc[(c, E * u + e)][:],
-                scalar1=be1_sb[:, c, u, e : e + 1],
+                out=h_plain[(c, a)][:, e, :],
+                in0=acc[(c, t)][:],
+                scalar1=be1_sb[:, c, t : t + 1],
                 scalar2=0.0,
                 op0=ALU.add,
                 op1=ALU.max,
             )
 
-        def h_copy(c, u):
+        def h_copy(c, a):
             nc.vector.tensor_copy(
-                out=h_grouped[c][:, :, E * u : E * u + E], in_=h_plain[(c, u)][:].rearrange("p e b -> p b e")
+                out=h_grouped[c][:, :, E * a : E * a + E], in_=h_plain[(c, a)][:].rearrange("p e b -> p b e")
             )
 
         def h_quantise(c):
@@ -192,26 +193,10 @@ def tile_vae_pa_s_kernel(tc, x, eps, We1, be1, Wmu, bmu, Wls, bls, out_0, out_1)
                 in_=h_grouped[c][:].rearrange("p b t -> p (b t)"),
             )
 
-        for c in range(C):
-            h_grouped[c] = keep.tile([P, BATCH, PACK], BF16, name="h_grouped%d" % c, align_bytes=64)
-            h_codes[c] = keep.tile([P, BATCH], U32, name="h_codes%d" % c, align_bytes=64)
-            h_scales[c] = keep.tile([P, BATCH], U8, name="h_scales%d" % c, align_bytes=64)
-            for u in range(U):
-                h_plain[(c, u)] = keep.tile([P, E, BATCH], BF16, name="h_plain%d%d" % (c, u))
-
-        head_grouped, head_codes, head_scales = {}, {}, {}
-        for head in (LS, MU):
-            head_grouped[head] = keep.tile([P, C, LATENT, PACK], BF16, name="head_grouped%d" % head, align_bytes=64)
-            head_codes[head] = keep.tile([P, C, LATENT], U32, name="head_codes%d" % head, align_bytes=64)
-            head_scales[head] = keep.tile([P, C, LATENT], U8, name="head_scales%d" % head, align_bytes=64)
-        head_raw = {LS: ls_raw, MU: mu_raw}
-
         def head_copy(copy, head, c, lo, hi):
-            src = head_raw[head][:, c].rearrange("p u (e l) -> p (u e) l", e=E)[:, :, lo:hi]
-            dst = head_grouped[head][:, c, lo:hi, :]
             copy(
-                out=dst.rearrange("p (n i) t -> p n t i", i=4),
-                in_=src.rearrange("p t (n i) -> p n t i", i=4),
+                out=head_grouped[head][:, c, lo:hi, :].rearrange("p (n i) t -> p n t i", i=4),
+                in_=head_raw[head][:, c, :, lo:hi].rearrange("p t (n i) -> p n t i", i=4),
             )
 
         def head_quantise(head):
@@ -220,8 +205,6 @@ def tile_vae_pa_s_kernel(tc, x, eps, We1, be1, Wmu, bmu, Wls, bls, out_0, out_1)
                 scales=head_scales[head][:].rearrange("p c l -> p (c l)"),
                 in_=head_grouped[head][:].rearrange("p c l t -> p (c l t)"),
             )
-
-        sums = {}
 
         def head_matmul(head, c):
             if c == 0:
@@ -236,46 +219,40 @@ def tile_vae_pa_s_kernel(tc, x, eps, We1, be1, Wmu, bmu, Wls, bls, out_0, out_1)
                 stop=(c == C - 1),
             )
 
-        w_copy((0, 0, 0))
-        w_copy((0, 0, 1))
-        w_quantise((0, 0, 0))
-        x_transposes()
-        nc.tensor.transpose(out=be1_t[:], in_=be1_rows[:].bitcast(F32), identity=ident[:])
-        x_copy()
-        nc.scalar.copy(out=be1_words[:], in_=be1_t[:, 0 : C * U])
-        w_copy((0, 1, 0))
-        w_quantise((0, 0, 1))
-        x_quantise()
-        w_matmul((0, 0, 0))
-        w_matmul((0, 0, 1))
-        w_copy((0, 1, 1))
-        w_quantise((0, 1, 0))
-        w_matmul((0, 1, 0))
         head_copy(nc.vector.tensor_copy, LS, 0, 0, LATENT)
-        head_copy(nc.scalar.copy, LS, 1, 0, LATENT)
-        w_quantise((0, 1, 1))
-        w_matmul((0, 1, 1))
-        relu_scalar(0, 0, 0)
-        relu_scalar(0, 0, 1)
-        w_copy((1, 0, 0))
+        head_copy(nc.scalar.copy, LS, 1, V_LATENT, LATENT)
+        head_copy(nc.vector.tensor_copy, LS, 1, 0, V_LATENT)
+        w_copy(0, 0, 0)
         head_quantise(LS)
-        relu_scalar(0, 1, 0)
-        relu_scalar(0, 1, 1)
-        w_copy((1, 0, 1))
-        w_quantise((1, 0, 0))
-        w_matmul((1, 0, 0))
-        h_copy(0, 0)
-        h_copy(0, 1)
-        w_copy((1, 1, 0))
-        w_quantise((1, 0, 1))
-        w_matmul((1, 0, 1))
-        h_quantise(0)
-        head_matmul(LS, 0)
-        w_copy((1, 1, 1))
-        w_quantise((1, 1, 0))
-        w_matmul((1, 1, 0))
-        w_quantise((1, 1, 1))
-        w_matmul((1, 1, 1))
+        w_copy(0, 0, 1)
+        w_quantise(0, 0, 0)
+        x_transposes()
+        x_copy()
+        w_copy(0, 1, 0)
+        w_quantise(0, 0, 1)
+        x_quantise()
+        w_matmul(0, 0, 0)
+        w_matmul(0, 0, 1)
+        w_copy(0, 1, 1)
+        w_quantise(0, 1, 0)
+        w_matmul(0, 1, 0)
+        w_copy(1, 0, 0)
+        w_quantise(0, 1, 1)
+        w_matmul(0, 1, 1)
+        w_copy(1, 0, 1)
+        w_quantise(1, 0, 0)
+        w_matmul(1, 0, 0)
+        for a in range(A):
+            for e in range(E):
+                relu_scalar(0, a, e)
+        w_copy(1, 1, 0)
+        w_quantise(1, 0, 1)
+        w_matmul(1, 0, 1)
+        w_copy(1, 1, 1)
+        w_quantise(1, 1, 0)
+        w_matmul(1, 1, 0)
+        w_quantise(1, 1, 1)
+        w_matmul(1, 1, 1)
         head_bias_ps = bank("head_bias_ps", 2, [P, 2, LATENT])
         nc.tensor.matmul(
             out=head_bias_ps[:].rearrange("p h l -> p (h l)"),
@@ -284,19 +261,23 @@ def tile_vae_pa_s_kernel(tc, x, eps, We1, be1, Wmu, bmu, Wls, bls, out_0, out_1)
             start=True,
             stop=True,
         )
-        head_copy(nc.scalar.copy, MU, 0, 0, LATENT // 2)
+        head_bias = keep.tile([P, 2, LATENT], F32)
+        h_copy(0, 0)
+        h_copy(0, 1)
+        h_quantise(0)
+        head_matmul(LS, 0)
+        head_copy(nc.scalar.copy, MU, 0, 0, 64)
         relu_scalar(1, 0, 0)
-        relu_vector(1, 0, 1)
-        head_copy(nc.scalar.copy, MU, 0, LATENT // 2, LATENT)
-        h_copy(1, 0)
+        relu_scalar(1, 0, 1)
         relu_scalar(1, 1, 0)
         relu_vector(1, 1, 1)
-        head_bias = keep.tile([P, 2, LATENT], F32)
-        nc.scalar.copy(out=head_bias[:], in_=head_bias_ps[:])
-        head_copy(nc.scalar.copy, MU, 1, 0, LATENT)
+        head_copy(nc.scalar.copy, MU, 0, 64, LATENT)
+        h_copy(1, 0)
         h_copy(1, 1)
         h_quantise(1)
         head_matmul(LS, 1)
+        nc.scalar.copy(out=head_bias[:], in_=head_bias_ps[:])
+        head_copy(nc.scalar.copy, MU, 1, 0, LATENT)
 
         log_sigma = keep.tile([P, LATENT], F32)
         sum_log_sigma = keep.tile([P, 1], F32)

@@ -25,7 +25,7 @@ A = 2
 E = 2
 MU, LS = 0, 1
 
-V_WORDS = 68
+V_WORDS = 66
 V_LATENT = 64
 
 FLOPS = 2 * BATCH * D_IN * HIDDEN + 2 * 2 * BATCH * HIDDEN * LATENT
@@ -69,8 +69,8 @@ def tile_vae_pa_s_kernel(tc, x, eps, We1, be1, Wmu, bmu, Wls, bls, out_0, out_1)
         x_sb = keep.tile([P, D_IN], BF16)
         eps_sb = keep.tile([P, LATENT], BF16)
         load_head(LS, Wls)
-        load_w(0, 0)
         nc.sync.dma_start(out=x_sb[:], in_=x)
+        load_w(0, 0)
         load_w(0, 1)
         load_w(1, 0)
         load_w(1, 1)
@@ -103,8 +103,7 @@ def tile_vae_pa_s_kernel(tc, x, eps, We1, be1, Wmu, bmu, Wls, bls, out_0, out_1)
             h_grouped[c] = keep.tile([P, BATCH, PACK], BF16, name="h_grouped%d" % c, align_bytes=64)
             h_codes[c] = keep.tile([P, BATCH], U32, name="h_codes%d" % c, align_bytes=64)
             h_scales[c] = keep.tile([P, BATCH], U8, name="h_scales%d" % c, align_bytes=64)
-            for a in range(A):
-                h_plain[(c, a)] = keep.tile([P, E, BATCH], BF16, name="h_plain%d%d" % (c, a))
+            h_plain[c] = keep.tile([P, PACK, BATCH], BF16, name="h_plain%d" % c)
             for g in range(G):
                 for a in range(A):
                     tag = "%d%d%d" % (c, g, a)
@@ -167,13 +166,13 @@ def tile_vae_pa_s_kernel(tc, x, eps, We1, be1, Wmu, bmu, Wls, bls, out_0, out_1)
         def relu_scalar(c, a, e):
             t = E * a + e
             nc.scalar.activation(
-                out=h_plain[(c, a)][:, e, :], in_=acc[(c, t)][:], func=ACT.Relu, bias=be1_sb[:, c, t : t + 1]
+                out=h_plain[c][:, t, :], in_=acc[(c, t)][:], func=ACT.Relu, bias=be1_sb[:, c, t : t + 1]
             )
 
         def relu_vector(c, a, e):
             t = E * a + e
             nc.vector.tensor_scalar(
-                out=h_plain[(c, a)][:, e, :],
+                out=h_plain[c][:, t, :],
                 in0=acc[(c, t)][:],
                 scalar1=be1_sb[:, c, t : t + 1],
                 scalar2=0.0,
@@ -181,9 +180,10 @@ def tile_vae_pa_s_kernel(tc, x, eps, We1, be1, Wmu, bmu, Wls, bls, out_0, out_1)
                 op1=ALU.max,
             )
 
-        def h_copy(c, a):
+        def h_copy(c):
             nc.vector.tensor_copy(
-                out=h_grouped[c][:, :, E * a : E * a + E], in_=h_plain[(c, a)][:].rearrange("p e b -> p b e")
+                out=h_grouped[c][:].rearrange("p (n i) t -> p n t i", i=4),
+                in_=h_plain[c][:].rearrange("p t (n i) -> p n t i", i=4),
             )
 
         def h_quantise(c):
@@ -222,37 +222,24 @@ def tile_vae_pa_s_kernel(tc, x, eps, We1, be1, Wmu, bmu, Wls, bls, out_0, out_1)
         head_copy(nc.vector.tensor_copy, LS, 0, 0, LATENT)
         head_copy(nc.scalar.copy, LS, 1, V_LATENT, LATENT)
         head_copy(nc.vector.tensor_copy, LS, 1, 0, V_LATENT)
-        w_copy(0, 0, 0)
-        head_quantise(LS)
-        w_copy(0, 0, 1)
-        w_quantise(0, 0, 0)
         x_transposes()
         x_copy()
-        w_copy(0, 1, 0)
-        w_quantise(0, 0, 1)
+        head_quantise(LS)
         x_quantise()
-        w_matmul(0, 0, 0)
-        w_matmul(0, 0, 1)
-        w_copy(0, 1, 1)
-        w_quantise(0, 1, 0)
-        w_matmul(0, 1, 0)
-        w_copy(1, 0, 0)
-        w_quantise(0, 1, 1)
-        w_matmul(0, 1, 1)
-        w_copy(1, 0, 1)
-        w_quantise(1, 0, 0)
-        w_matmul(1, 0, 0)
+        for c, g in ((0, 0), (0, 1), (1, 0)):
+            for a in range(A):
+                w_copy(c, g, a)
+            for a in range(A):
+                w_quantise(c, g, a)
+                w_matmul(c, g, a)
         for a in range(A):
             for e in range(E):
                 relu_scalar(0, a, e)
-        w_copy(1, 1, 0)
-        w_quantise(1, 0, 1)
-        w_matmul(1, 0, 1)
-        w_copy(1, 1, 1)
-        w_quantise(1, 1, 0)
-        w_matmul(1, 1, 0)
-        w_quantise(1, 1, 1)
-        w_matmul(1, 1, 1)
+        for a in range(A):
+            w_copy(1, 1, a)
+        for a in range(A):
+            w_quantise(1, 1, a)
+            w_matmul(1, 1, a)
         head_bias_ps = bank("head_bias_ps", 2, [P, 2, LATENT])
         nc.tensor.matmul(
             out=head_bias_ps[:].rearrange("p h l -> p (h l)"),
@@ -261,23 +248,24 @@ def tile_vae_pa_s_kernel(tc, x, eps, We1, be1, Wmu, bmu, Wls, bls, out_0, out_1)
             start=True,
             stop=True,
         )
-        head_bias = keep.tile([P, 2, LATENT], F32)
-        h_copy(0, 0)
-        h_copy(0, 1)
+        h_copy(0)
         h_quantise(0)
         head_matmul(LS, 0)
-        head_copy(nc.scalar.copy, MU, 0, 0, 64)
+        head_copy(nc.scalar.copy, MU, 0, 0, LATENT // 2)
         relu_scalar(1, 0, 0)
         relu_scalar(1, 0, 1)
         relu_scalar(1, 1, 0)
         relu_vector(1, 1, 1)
-        head_copy(nc.scalar.copy, MU, 0, 64, LATENT)
-        h_copy(1, 0)
-        h_copy(1, 1)
+        head_copy(nc.scalar.copy, MU, 0, LATENT // 2, LATENT)
+        head_copy(nc.scalar.copy, MU, 1, 0, LATENT)
+        head_bias = keep.tile([P, 2, LATENT], F32)
+        nc.scalar.copy(out=head_bias[:], in_=head_bias_ps[:])
+        h_copy(1)
         h_quantise(1)
         head_matmul(LS, 1)
-        nc.scalar.copy(out=head_bias[:], in_=head_bias_ps[:])
-        head_copy(nc.scalar.copy, MU, 1, 0, LATENT)
+        head_quantise(MU)
+        head_matmul(MU, 0)
+        head_matmul(MU, 1)
 
         log_sigma = keep.tile([P, LATENT], F32)
         sum_log_sigma = keep.tile([P, 1], F32)
@@ -290,36 +278,33 @@ def tile_vae_pa_s_kernel(tc, x, eps, We1, be1, Wmu, bmu, Wls, bls, out_0, out_1)
             op1=ALU.add,
             accum_out=sum_log_sigma[:],
         )
-        sigma = keep.tile([P, LATENT], F32)
-        nc.scalar.activation(out=sigma[:], in_=log_sigma[:], func=ACT.Exp)
-        head_quantise(MU)
-        head_matmul(MU, 0)
-        head_matmul(MU, 1)
-        noise = keep.tile([P, LATENT], F32)
-        nc.vector.tensor_tensor(out=noise[:], in0=sigma[:], in1=eps_sb[:], op=ALU.mult)
         mu = keep.tile([P, LATENT], F32)
         nc.vector.tensor_tensor(out=mu[:], in0=sums[MU][:], in1=head_bias[:, MU, :], op=ALU.add)
-        sigma_sq = keep.tile([P, LATENT], F32)
-        sum_sigma_sq = keep.tile([P, 1], F32)
-        nc.scalar.activation(out=sigma_sq[:], in_=log_sigma[:], func=ACT.Exp, scale=2.0, accum_out=sum_sigma_sq[:])
+        sigma = keep.tile([P, LATENT], F32)
+        nc.scalar.activation(out=sigma[:], in_=log_sigma[:], func=ACT.Exp)
         mu_sq = keep.tile([P, LATENT], F32)
         half_mu_sq = keep.tile([P, 1], F32)
         nc.scalar.activation(out=mu_sq[:], in_=mu[:], func=ACT.Square, scale=0.5**0.5, accum_out=half_mu_sq[:])
-        part = keep.tile([P, 1], F32)
-        half_sigma_sq = keep.tile([P, 1], F32)
+        sigma_sq = keep.tile([P, LATENT], F32)
+        sum_sigma_sq = keep.tile([P, 1], F32)
+        nc.scalar.activation(out=sigma_sq[:], in_=log_sigma[:], func=ACT.Exp, scale=2.0, accum_out=sum_sigma_sq[:])
+        noise = keep.tile([P, LATENT], F32)
+        nc.vector.tensor_tensor(out=noise[:], in0=sigma[:], in1=eps_sb[:], op=ALU.mult)
+        kl_rest = keep.tile([P, 1], F32)
         nc.vector.tensor_scalar(
-            out=half_sigma_sq[:],
-            in0=sum_sigma_sq[:],
-            scalar1=0.5,
+            out=kl_rest[:],
+            in0=half_mu_sq[:],
+            scalar1=sum_log_sigma[:],
             scalar2=-0.5 * LATENT,
-            op0=ALU.mult,
+            op0=ALU.subtract,
             op1=ALU.add,
         )
         z = keep.tile([P, LATENT], F32)
         nc.vector.tensor_tensor(out=z[:], in0=noise[:], in1=mu[:], op=ALU.add)
         nc.sync.dma_start(out=out_0, in_=z[:])
-        nc.vector.tensor_tensor(out=part[:], in0=half_sigma_sq[:], in1=sum_log_sigma[:], op=ALU.subtract)
-        nc.vector.tensor_tensor(out=kl_cols[:, 0:1], in0=half_mu_sq[:], in1=part[:], op=ALU.add)
+        nc.vector.scalar_tensor_tensor(
+            out=kl_cols[:, 0:1], in0=sum_sigma_sq[:], scalar=0.5, in1=kl_rest[:], op0=ALU.mult, op1=ALU.add
+        )
         kl_rows = keep.tile([P, 32], F32, align_bytes=64)
         nc.vector.transpose(kl_rows[:], kl_cols[:])
         nc.scalar.dma_start(out=out_1.rearrange("(a b) -> a b", b=32), in_=kl_rows[0:P:32, :])

@@ -69,8 +69,8 @@ def tile_vae_pa_s_kernel(tc, x, eps, We1, be1, Wmu, bmu, Wls, bls, out_0, out_1)
         x_sb = keep.tile([P, D_IN], BF16)
         eps_sb = keep.tile([P, LATENT], BF16)
         load_head(LS, Wls)
-        nc.sync.dma_start(out=x_sb[:], in_=x)
         load_w(0, 0)
+        nc.sync.dma_start(out=x_sb[:], in_=x)
         load_w(0, 1)
         load_w(1, 0)
         load_w(1, 1)
@@ -88,8 +88,8 @@ def tile_vae_pa_s_kernel(tc, x, eps, We1, be1, Wmu, bmu, Wls, bls, out_0, out_1)
         table_out = keep.tile([P, 1], F32)
         nc.scalar.activation(out=table_out[:], in_=table_in[:], func=ACT.Exp)
 
-        def bank(name, index, shape):
-            return psum.tile(shape, F32, name=name, tag="bank%d" % index)
+        def bank(name, index, shape, dtype=F32):
+            return psum.tile(shape, dtype, name=name, tag="bank%d" % index)
 
         x_t = bank("x_t", 7, [P, G, 2, BATCH])
         acc = {}
@@ -222,16 +222,27 @@ def tile_vae_pa_s_kernel(tc, x, eps, We1, be1, Wmu, bmu, Wls, bls, out_0, out_1)
         head_copy(nc.vector.tensor_copy, LS, 0, 0, LATENT)
         head_copy(nc.scalar.copy, LS, 1, V_LATENT, LATENT)
         head_copy(nc.vector.tensor_copy, LS, 1, 0, V_LATENT)
+        head_quantise(LS)
+        w_copy(0, 0, 0)
+        w_copy(0, 0, 1)
         x_transposes()
         x_copy()
-        head_quantise(LS)
+        w_quantise(0, 0, 0)
+        w_quantise(0, 0, 1)
+        w_copy(0, 1, 0)
         x_quantise()
-        for c, g in ((0, 0), (0, 1), (1, 0)):
-            for a in range(A):
-                w_copy(c, g, a)
-            for a in range(A):
-                w_quantise(c, g, a)
-                w_matmul(c, g, a)
+        w_matmul(0, 0, 0)
+        w_matmul(0, 0, 1)
+        w_copy(0, 1, 1)
+        w_quantise(0, 1, 0)
+        w_matmul(0, 1, 0)
+        w_quantise(0, 1, 1)
+        w_matmul(0, 1, 1)
+        for a in range(A):
+            w_copy(1, 0, a)
+        for a in range(A):
+            w_quantise(1, 0, a)
+            w_matmul(1, 0, a)
         for a in range(A):
             for e in range(E):
                 relu_scalar(0, a, e)
@@ -240,7 +251,7 @@ def tile_vae_pa_s_kernel(tc, x, eps, We1, be1, Wmu, bmu, Wls, bls, out_0, out_1)
         for a in range(A):
             w_quantise(1, 1, a)
             w_matmul(1, 1, a)
-        head_bias_ps = bank("head_bias_ps", 2, [P, 2, LATENT])
+        head_bias_ps = bank("head_bias_ps", 2, [P, 2, LATENT], BF16)
         nc.tensor.matmul(
             out=head_bias_ps[:].rearrange("p h l -> p (h l)"),
             lhsT=ones[:],
@@ -258,7 +269,7 @@ def tile_vae_pa_s_kernel(tc, x, eps, We1, be1, Wmu, bmu, Wls, bls, out_0, out_1)
         relu_vector(1, 1, 1)
         head_copy(nc.scalar.copy, MU, 0, LATENT // 2, LATENT)
         head_copy(nc.scalar.copy, MU, 1, 0, LATENT)
-        head_bias = keep.tile([P, 2, LATENT], F32)
+        head_bias = keep.tile([P, 2, LATENT], BF16)
         nc.scalar.copy(out=head_bias[:], in_=head_bias_ps[:])
         h_copy(1)
         h_quantise(1)
@@ -282,28 +293,33 @@ def tile_vae_pa_s_kernel(tc, x, eps, We1, be1, Wmu, bmu, Wls, bls, out_0, out_1)
         nc.vector.tensor_tensor(out=mu[:], in0=sums[MU][:], in1=head_bias[:, MU, :], op=ALU.add)
         sigma = keep.tile([P, LATENT], F32)
         nc.scalar.activation(out=sigma[:], in_=log_sigma[:], func=ACT.Exp)
-        mu_sq = keep.tile([P, LATENT], F32)
-        half_mu_sq = keep.tile([P, 1], F32)
-        nc.scalar.activation(out=mu_sq[:], in_=mu[:], func=ACT.Square, scale=0.5**0.5, accum_out=half_mu_sq[:])
         sigma_sq = keep.tile([P, LATENT], F32)
         sum_sigma_sq = keep.tile([P, 1], F32)
         nc.scalar.activation(out=sigma_sq[:], in_=log_sigma[:], func=ACT.Exp, scale=2.0, accum_out=sum_sigma_sq[:])
+        mu_sq = keep.tile([P, LATENT], F32)
+        half_mu_sq = keep.tile([P, 1], F32)
+        nc.scalar.activation(out=mu_sq[:], in_=mu[:], func=ACT.Square, scale=0.5**0.5, accum_out=half_mu_sq[:])
         noise = keep.tile([P, LATENT], F32)
         nc.vector.tensor_tensor(out=noise[:], in0=sigma[:], in1=eps_sb[:], op=ALU.mult)
-        kl_rest = keep.tile([P, 1], F32)
+        half_sigma_sq = keep.tile([P, 1], F32)
         nc.vector.tensor_scalar(
-            out=kl_rest[:],
-            in0=half_mu_sq[:],
-            scalar1=sum_log_sigma[:],
+            out=half_sigma_sq[:],
+            in0=sum_sigma_sq[:],
+            scalar1=0.5,
             scalar2=-0.5 * LATENT,
-            op0=ALU.subtract,
+            op0=ALU.mult,
             op1=ALU.add,
         )
         z = keep.tile([P, LATENT], F32)
         nc.vector.tensor_tensor(out=z[:], in0=noise[:], in1=mu[:], op=ALU.add)
         nc.sync.dma_start(out=out_0, in_=z[:])
-        nc.vector.scalar_tensor_tensor(
-            out=kl_cols[:, 0:1], in0=sum_sigma_sq[:], scalar=0.5, in1=kl_rest[:], op0=ALU.mult, op1=ALU.add
+        nc.vector.tensor_scalar(
+            out=kl_cols[:, 0:1],
+            in0=half_sigma_sq[:],
+            scalar1=half_mu_sq[:],
+            scalar2=sum_log_sigma[:],
+            op0=ALU.add,
+            op1=ALU.subtract,
         )
         kl_rows = keep.tile([P, 32], F32, align_bytes=64)
         nc.vector.transpose(kl_rows[:], kl_cols[:])

@@ -25,7 +25,7 @@ A = 2
 E = 2
 MU, LS = 0, 1
 
-V_WORDS = 66
+V_COLS = 144
 V_LATENT = 64
 
 FLOPS = 2 * BATCH * D_IN * HIDDEN + 2 * 2 * BATCH * HIDDEN * LATENT
@@ -38,8 +38,10 @@ def tile_vae_pa_s_kernel(tc, x, eps, We1, be1, Wmu, bmu, Wls, bls, out_0, out_1)
         psum = ctx.enter_context(tc.psum_pool(name="psum", bufs=1))
         ctx.enter_context(tc.manual_schedule())
 
+        be1_rows = keep.tile([P, P], BF16)
+        nc.vector.memset(be1_rows[:], 0.0)
+        nc.scalar.dma_start(out=be1_rows[0 : C * PACK, :], in_=be1.rearrange("(r w) -> r w", w=P))
         be1_sb = keep.tile([P, C, PACK], BF16)
-        nc.scalar.dma_start(out=be1_sb[:], in_=be1.rearrange("(c p t) -> p c t", c=C, t=PACK))
         head_bias_row = keep.tile([P, 2 * LATENT], BF16)
         nc.vector.memset(head_bias_row[:], 0.0)
         for head, bias in ((MU, bmu), (LS, bls)):
@@ -53,32 +55,38 @@ def tile_vae_pa_s_kernel(tc, x, eps, We1, be1, Wmu, bmu, Wls, bls, out_0, out_1)
         def load_head(head, weights):
             head_raw[head] = keep.tile([P, C, PACK, LATENT], BF16, name="head_raw%d" % head)
             nc.sync.dma_start(
-                out=head_raw[head][:].rearrange("p c t l -> p c (t l)"),
-                in_=weights.rearrange("(c p t) l -> p c (t l)", c=C, t=PACK),
+                out=head_raw[head][:],
+                in_=weights.rearrange("(c t p) l -> p c t l", c=C, t=PACK),
             )
 
-        def load_w(c, g):
-            w_raw[(c, g)] = keep.tile([P, PACK, K_PASS], BF16, name="w_raw%d%d" % (c, g))
+        def load_w(c, g, a0, units):
+            raw = keep.tile([P, PACK, units * E * P], BF16, name="w_raw%d%d%d" % (c, g, a0))
+            first = c * K_PASS + a0 * E * P
             nc.sync.dma_start(
-                out=w_raw[(c, g)][:],
-                in_=We1[g * K_PASS : (g + 1) * K_PASS, c * K_PASS : (c + 1) * K_PASS].rearrange(
+                out=raw[:],
+                in_=We1[g * K_PASS : (g + 1) * K_PASS, first : first + units * E * P].rearrange(
                     "(p j) w -> p j w", j=PACK
                 ),
             )
+            for i in range(units):
+                w_raw[(c, g, a0 + i)] = raw[:, :, i * E * P : (i + 1) * E * P]
 
         x_sb = keep.tile([P, D_IN], BF16)
         eps_sb = keep.tile([P, LATENT], BF16)
-        load_head(LS, Wls)
-        load_w(0, 0)
+        load_w(0, 0, 0, 1)
+        load_w(0, 0, 1, 1)
         nc.sync.dma_start(out=x_sb[:], in_=x)
-        load_w(0, 1)
-        load_w(1, 0)
-        load_w(1, 1)
+        load_w(0, 1, 0, A)
+        load_head(LS, Wls)
+        load_w(1, 0, 0, A)
+        load_w(1, 1, 0, A)
         load_head(MU, Wmu)
         nc.sync.dma_start(out=eps_sb[:], in_=eps)
 
         ident = keep.tile([P, P], F32)
         make_identity(nc, ident[:])
+        ident_bf = keep.tile([P, P], BF16)
+        nc.vector.tensor_copy(out=ident_bf[:], in_=ident[:])
         ones = keep.tile([P, P], BF16)
         nc.vector.memset(ones[:], 1.0)
         kl_cols = keep.tile([P, 32], F32, align_bytes=64)
@@ -135,10 +143,10 @@ def tile_vae_pa_s_kernel(tc, x, eps, We1, be1, Wmu, bmu, Wls, bls, out_0, out_1)
             )
 
         def w_copy(c, g, a):
-            src = w_raw[(c, g)][:].rearrange("p j (q a e) -> p a q j e", a=A, e=E)[:, a]
-            dst = w_grouped[(c, g, a)][:].rearrange("p e q j -> p q j e")
-            nc.vector.tensor_copy(out=dst[:, :V_WORDS], in_=src[:, :V_WORDS])
-            nc.scalar.copy(out=dst[:, V_WORDS:], in_=src[:, V_WORDS:])
+            src = w_raw[(c, g, a)].rearrange("p j (n i) -> p n j i", i=4)
+            dst = w_grouped[(c, g, a)][:].rearrange("p e (n i) j -> p (e n) j i", i=4)
+            nc.vector.tensor_copy(out=dst[:, : V_COLS // 4], in_=src[:, : V_COLS // 4])
+            nc.scalar.copy(out=dst[:, V_COLS // 4 :], in_=src[:, V_COLS // 4 :])
 
         def w_quantise(c, g, a):
             unit = (c, g, a)
@@ -199,11 +207,11 @@ def tile_vae_pa_s_kernel(tc, x, eps, We1, be1, Wmu, bmu, Wls, bls, out_0, out_1)
                 in_=head_raw[head][:, c, :, lo:hi].rearrange("p t (n i) -> p n t i", i=4),
             )
 
-        def head_quantise(head):
+        def head_quantise(head, c):
             nc.vector.quantize_mx(
-                out=head_codes[head][:].rearrange("p c l -> p (c l)").bitcast(FP8X4),
-                scales=head_scales[head][:].rearrange("p c l -> p (c l)"),
-                in_=head_grouped[head][:].rearrange("p c l t -> p (c l t)"),
+                out=head_codes[head][:, c, :].bitcast(FP8X4),
+                scales=head_scales[head][:, c, :],
+                in_=head_grouped[head][:, c].rearrange("p l t -> p (l t)"),
             )
 
         def head_matmul(head, c):
@@ -219,10 +227,6 @@ def tile_vae_pa_s_kernel(tc, x, eps, We1, be1, Wmu, bmu, Wls, bls, out_0, out_1)
                 stop=(c == C - 1),
             )
 
-        head_copy(nc.vector.tensor_copy, LS, 0, 0, LATENT)
-        head_copy(nc.scalar.copy, LS, 1, V_LATENT, LATENT)
-        head_copy(nc.vector.tensor_copy, LS, 1, 0, V_LATENT)
-        head_quantise(LS)
         w_copy(0, 0, 0)
         w_copy(0, 0, 1)
         x_transposes()
@@ -238,8 +242,16 @@ def tile_vae_pa_s_kernel(tc, x, eps, We1, be1, Wmu, bmu, Wls, bls, out_0, out_1)
         w_matmul(0, 1, 0)
         w_quantise(0, 1, 1)
         w_matmul(0, 1, 1)
+        be1_t = bank("be1_t", 7, [P, P], BF16)
+        nc.tensor.transpose(out=be1_t[:], in_=be1_rows[:], identity=ident_bf[:])
+        head_copy(nc.vector.tensor_copy, LS, 0, 0, LATENT)
+        head_copy(nc.scalar.copy, LS, 1, V_LATENT, LATENT)
+        head_copy(nc.vector.tensor_copy, LS, 1, 0, V_LATENT)
         for a in range(A):
             w_copy(1, 0, a)
+        for c in range(C):
+            head_quantise(LS, c)
+        nc.scalar.copy(out=be1_sb[:].rearrange("p c t -> p (c t)"), in_=be1_t[:, 0 : C * PACK])
         for a in range(A):
             w_quantise(1, 0, a)
             w_matmul(1, 0, a)
@@ -260,22 +272,23 @@ def tile_vae_pa_s_kernel(tc, x, eps, We1, be1, Wmu, bmu, Wls, bls, out_0, out_1)
             stop=True,
         )
         h_copy(0)
-        h_quantise(0)
-        head_matmul(LS, 0)
         head_copy(nc.scalar.copy, MU, 0, 0, LATENT // 2)
         relu_scalar(1, 0, 0)
         relu_scalar(1, 0, 1)
         relu_scalar(1, 1, 0)
         relu_vector(1, 1, 1)
+        h_quantise(0)
+        head_matmul(LS, 0)
         head_copy(nc.scalar.copy, MU, 0, LATENT // 2, LATENT)
         head_copy(nc.scalar.copy, MU, 1, 0, LATENT)
         head_bias = keep.tile([P, 2, LATENT], BF16)
         nc.scalar.copy(out=head_bias[:], in_=head_bias_ps[:])
         h_copy(1)
+        head_quantise(MU, 0)
         h_quantise(1)
         head_matmul(LS, 1)
-        head_quantise(MU)
         head_matmul(MU, 0)
+        head_quantise(MU, 1)
         head_matmul(MU, 1)
 
         log_sigma = keep.tile([P, LATENT], F32)

@@ -24,9 +24,9 @@ C = HIDDEN // K_PASS
 A = 2
 E = 2
 MU, LS = 0, 1
+BIAS_ROWS = 2
 
-V_COLS = 144
-V_LATENT = 64
+V_COLS = 152
 
 FLOPS = 2 * BATCH * D_IN * HIDDEN + 2 * 2 * BATCH * HIDDEN * LATENT
 
@@ -38,17 +38,21 @@ def tile_vae_pa_s_kernel(tc, x, eps, We1, be1, Wmu, bmu, Wls, bls, out_0, out_1)
         psum = ctx.enter_context(tc.psum_pool(name="psum", bufs=1))
         ctx.enter_context(tc.manual_schedule())
 
-        be1_rows = keep.tile([P, P], BF16)
-        nc.vector.memset(be1_rows[:], 0.0)
-        nc.scalar.dma_start(out=be1_rows[0 : C * PACK, :], in_=be1.rearrange("(r w) -> r w", w=P))
-        be1_sb = keep.tile([P, C, PACK], BF16)
-        head_bias_row = keep.tile([P, 2 * LATENT], BF16)
-        nc.vector.memset(head_bias_row[:], 0.0)
+        table_in = keep.tile([P, 1], F32)
+        nc.vector.memset(table_in[:], 0.0)
+        table_out = keep.tile([P, 1], F32)
+        nc.scalar.activation(out=table_out[:], in_=table_in[:], func=ACT.Exp)
+
+        rows = keep.tile([P, P], BF16)
+        nc.vector.memset(rows[:], 0.0)
+        nc.scalar.dma_start(out=rows[0 : C * PACK, :], in_=be1.rearrange("(r w) -> r w", w=P))
+        first_bias_row = {MU: C * PACK, LS: C * PACK + BIAS_ROWS}
         for head, bias in ((MU, bmu), (LS, bls)):
             nc.scalar.dma_start(
-                out=head_bias_row[0:1, head * LATENT : (head + 1) * LATENT],
-                in_=bias.rearrange("(o l) -> o l", o=1),
+                out=rows[first_bias_row[head] : first_bias_row[head] + BIAS_ROWS, 0 : LATENT // BIAS_ROWS],
+                in_=bias.rearrange("(r w) -> r w", r=BIAS_ROWS),
             )
+        be1_sb = keep.tile([P, C, PACK], BF16)
 
         head_raw, w_raw = {}, {}
 
@@ -87,14 +91,10 @@ def tile_vae_pa_s_kernel(tc, x, eps, We1, be1, Wmu, bmu, Wls, bls, out_0, out_1)
         make_identity(nc, ident[:])
         ident_bf = keep.tile([P, P], BF16)
         nc.vector.tensor_copy(out=ident_bf[:], in_=ident[:])
-        ones = keep.tile([P, P], BF16)
-        nc.vector.memset(ones[:], 1.0)
         kl_cols = keep.tile([P, 32], F32, align_bytes=64)
         nc.vector.memset(kl_cols[:], 0.0)
-        table_in = keep.tile([P, 1], F32)
-        nc.vector.memset(table_in[:], 0.0)
-        table_out = keep.tile([P, 1], F32)
-        nc.scalar.activation(out=table_out[:], in_=table_in[:], func=ACT.Exp)
+        half = keep.tile([P, 1], F32)
+        nc.vector.memset(half[:], 0.5)
 
         def bank(name, index, shape, dtype=F32):
             return psum.tile(shape, dtype, name=name, tag="bank%d" % index)
@@ -156,8 +156,16 @@ def tile_vae_pa_s_kernel(tc, x, eps, We1, be1, Wmu, bmu, Wls, bls, out_0, out_1)
                 in_=w_grouped[unit][:].rearrange("p e q j -> p (e q j)"),
             )
 
-        def w_matmul(c, g, a):
-            for e in range(E):
+        def tile_quantise(c, g, a, e):
+            unit = (c, g, a)
+            nc.vector.quantize_mx(
+                out=w_codes[unit][:, e, :].bitcast(FP8X4),
+                scales=w_scales[unit][:, e, :],
+                in_=w_grouped[unit][:, e].rearrange("p q j -> p (q j)"),
+            )
+
+        def w_matmul(c, g, a, tiles=range(E)):
+            for e in tiles:
                 t = E * a + e
                 if g == 0:
                     acc[(c, t)] = bank("acc%d%d" % (c, t), 4 * c + t, [P, BATCH])
@@ -243,10 +251,9 @@ def tile_vae_pa_s_kernel(tc, x, eps, We1, be1, Wmu, bmu, Wls, bls, out_0, out_1)
         w_quantise(0, 1, 1)
         w_matmul(0, 1, 1)
         be1_t = bank("be1_t", 7, [P, P], BF16)
-        nc.tensor.transpose(out=be1_t[:], in_=be1_rows[:], identity=ident_bf[:])
+        nc.tensor.transpose(out=be1_t[:], in_=rows[:], identity=ident_bf[:])
         head_copy(nc.vector.tensor_copy, LS, 0, 0, LATENT)
-        head_copy(nc.scalar.copy, LS, 1, V_LATENT, LATENT)
-        head_copy(nc.vector.tensor_copy, LS, 1, 0, V_LATENT)
+        head_copy(nc.scalar.copy, LS, 1, 0, LATENT)
         for a in range(A):
             w_copy(1, 0, a)
         for c in range(C):
@@ -260,77 +267,75 @@ def tile_vae_pa_s_kernel(tc, x, eps, We1, be1, Wmu, bmu, Wls, bls, out_0, out_1)
                 relu_scalar(0, a, e)
         for a in range(A):
             w_copy(1, 1, a)
-        for a in range(A):
-            w_quantise(1, 1, a)
-            w_matmul(1, 1, a)
+        w_quantise(1, 1, 0)
+        w_matmul(1, 1, 0)
+        for e in range(E):
+            tile_quantise(1, 1, 1, e)
+            w_matmul(1, 1, 1, (e,))
         head_bias_ps = bank("head_bias_ps", 2, [P, 2, LATENT], BF16)
-        nc.tensor.matmul(
-            out=head_bias_ps[:].rearrange("p h l -> p (h l)"),
-            lhsT=ones[:],
-            rhs=head_bias_row[:],
-            start=True,
-            stop=True,
-        )
+        for head in (MU, LS):
+            for r in range(BIAS_ROWS):
+                row = first_bias_row[head] + r
+                width = LATENT // BIAS_ROWS
+                nc.tensor.matmul(
+                    out=head_bias_ps[:, head, r * width : (r + 1) * width],
+                    lhsT=ident_bf[:, row : row + 1].to_broadcast([P, P]),
+                    rhs=rows[:, 0:width],
+                    start=True,
+                    stop=True,
+                )
         h_copy(0)
-        head_copy(nc.scalar.copy, MU, 0, 0, LATENT // 2)
+        head_copy(nc.scalar.copy, MU, 0, 0, LATENT)
         relu_scalar(1, 0, 0)
         relu_scalar(1, 0, 1)
+        head_quantise(MU, 0)
         relu_scalar(1, 1, 0)
         relu_vector(1, 1, 1)
         h_quantise(0)
         head_matmul(LS, 0)
-        head_copy(nc.scalar.copy, MU, 0, LATENT // 2, LATENT)
-        head_copy(nc.scalar.copy, MU, 1, 0, LATENT)
+        head_matmul(MU, 0)
         head_bias = keep.tile([P, 2, LATENT], BF16)
         nc.scalar.copy(out=head_bias[:], in_=head_bias_ps[:])
+        head_copy(nc.scalar.copy, MU, 1, 0, LATENT)
         h_copy(1)
-        head_quantise(MU, 0)
         h_quantise(1)
         head_matmul(LS, 1)
-        head_matmul(MU, 0)
         head_quantise(MU, 1)
         head_matmul(MU, 1)
 
         log_sigma = keep.tile([P, LATENT], F32)
-        sum_log_sigma = keep.tile([P, 1], F32)
-        nc.vector.scalar_tensor_tensor(
-            out=log_sigma[:],
-            in0=sums[LS][:],
-            scalar=1.0,
-            in1=head_bias[:, LS, :],
-            op0=ALU.mult,
-            op1=ALU.add,
-            accum_out=sum_log_sigma[:],
-        )
+        nc.vector.tensor_tensor(out=log_sigma[:], in0=sums[LS][:], in1=head_bias[:, LS, :], op=ALU.add)
         mu = keep.tile([P, LATENT], F32)
         nc.vector.tensor_tensor(out=mu[:], in0=sums[MU][:], in1=head_bias[:, MU, :], op=ALU.add)
         sigma = keep.tile([P, LATENT], F32)
         nc.scalar.activation(out=sigma[:], in_=log_sigma[:], func=ACT.Exp)
-        sigma_sq = keep.tile([P, LATENT], F32)
-        sum_sigma_sq = keep.tile([P, 1], F32)
-        nc.scalar.activation(out=sigma_sq[:], in_=log_sigma[:], func=ACT.Exp, scale=2.0, accum_out=sum_sigma_sq[:])
-        mu_sq = keep.tile([P, LATENT], F32)
-        half_mu_sq = keep.tile([P, 1], F32)
-        nc.scalar.activation(out=mu_sq[:], in_=mu[:], func=ACT.Square, scale=0.5**0.5, accum_out=half_mu_sq[:])
         noise = keep.tile([P, LATENT], F32)
         nc.vector.tensor_tensor(out=noise[:], in0=sigma[:], in1=eps_sb[:], op=ALU.mult)
-        half_sigma_sq = keep.tile([P, 1], F32)
-        nc.vector.tensor_scalar(
-            out=half_sigma_sq[:],
-            in0=sum_sigma_sq[:],
-            scalar1=0.5,
-            scalar2=-0.5 * LATENT,
-            op0=ALU.mult,
-            op1=ALU.add,
-        )
+        terms = keep.tile([P, 3, LATENT], F32)
+        kl_sums = keep.tile([P, 3], F32)
+        for i, (values, func, scale, bias) in enumerate(
+            (
+                (sigma, ACT.Square, 0.5**0.5, 0.0),
+                (log_sigma, ACT.Identity, 1.0, half[:]),
+                (mu, ACT.Square, 0.5**0.5, 0.0),
+            )
+        ):
+            nc.scalar.activation(
+                out=terms[:, i, :],
+                in_=values[:],
+                func=func,
+                scale=scale,
+                bias=bias,
+                accum_out=kl_sums[:, i : i + 1],
+            )
         z = keep.tile([P, LATENT], F32)
         nc.vector.tensor_tensor(out=z[:], in0=noise[:], in1=mu[:], op=ALU.add)
         nc.sync.dma_start(out=out_0, in_=z[:])
         nc.vector.tensor_scalar(
             out=kl_cols[:, 0:1],
-            in0=half_sigma_sq[:],
-            scalar1=half_mu_sq[:],
-            scalar2=sum_log_sigma[:],
+            in0=kl_sums[:, 0:1],
+            scalar1=kl_sums[:, 2:3],
+            scalar2=kl_sums[:, 1:2],
             op0=ALU.add,
             op1=ALU.subtract,
         )

from contextlib import ExitStack

import concourse.mybir as mybir
from concourse.masks import make_identity

F32 = mybir.dt.float32
BF16 = mybir.dt.bfloat16
U32 = mybir.dt.uint32
U8 = mybir.dt.uint8
FP8X4 = mybir.dt.float8_e4m3fn_x4
ACT = mybir.ActivationFunctionType
ALU = mybir.AluOpType

P = 128
PACK = 4
K_PASS = P * PACK

BATCH = 128
D_IN = 1024
HIDDEN = 1024
LATENT = 128
G = D_IN // K_PASS
C = HIDDEN // K_PASS
A = 2
E = 2
MU, LS = 0, 1
BIAS_ROWS = 2

V_COLS = 152

FLOPS = 2 * BATCH * D_IN * HIDDEN + 2 * 2 * BATCH * HIDDEN * LATENT


def tile_vae_pa_s_kernel(tc, x, eps, We1, be1, Wmu, bmu, Wls, bls, out_0, out_1):
    nc = tc.nc
    with ExitStack() as ctx:
        keep = ctx.enter_context(tc.tile_pool(name="keep", bufs=1))
        psum = ctx.enter_context(tc.psum_pool(name="psum", bufs=1))
        ctx.enter_context(tc.manual_schedule())

        table_in = keep.tile([P, 1], F32)
        nc.vector.memset(table_in[:], 0.0)
        table_out = keep.tile([P, 1], F32)
        nc.scalar.activation(out=table_out[:], in_=table_in[:], func=ACT.Exp)

        rows = keep.tile([P, P], BF16)
        nc.vector.memset(rows[:], 0.0)
        nc.scalar.dma_start(out=rows[0 : C * PACK, :], in_=be1.rearrange("(r w) -> r w", w=P))
        first_bias_row = {MU: C * PACK, LS: C * PACK + BIAS_ROWS}
        for head, bias in ((MU, bmu), (LS, bls)):
            nc.scalar.dma_start(
                out=rows[first_bias_row[head] : first_bias_row[head] + BIAS_ROWS, 0 : LATENT // BIAS_ROWS],
                in_=bias.rearrange("(r w) -> r w", r=BIAS_ROWS),
            )
        be1_sb = keep.tile([P, C, PACK], BF16)

        head_raw, w_raw = {}, {}

        def load_head(head, weights):
            head_raw[head] = keep.tile([P, C, PACK, LATENT], BF16, name="head_raw%d" % head)
            nc.sync.dma_start(
                out=head_raw[head][:],
                in_=weights.rearrange("(c t p) l -> p c t l", c=C, t=PACK),
            )

        def load_w(c, g, a0, units):
            raw = keep.tile([P, PACK, units * E * P], BF16, name="w_raw%d%d%d" % (c, g, a0))
            first = c * K_PASS + a0 * E * P
            nc.sync.dma_start(
                out=raw[:],
                in_=We1[g * K_PASS : (g + 1) * K_PASS, first : first + units * E * P].rearrange(
                    "(p j) w -> p j w", j=PACK
                ),
            )
            for i in range(units):
                w_raw[(c, g, a0 + i)] = raw[:, :, i * E * P : (i + 1) * E * P]

        x_sb = keep.tile([P, D_IN], BF16)
        eps_sb = keep.tile([P, LATENT], BF16)
        load_w(0, 0, 0, 1)
        load_w(0, 0, 1, 1)
        nc.sync.dma_start(out=x_sb[:], in_=x)
        load_w(0, 1, 0, A)
        load_head(LS, Wls)
        load_w(1, 0, 0, A)
        load_w(1, 1, 0, A)
        load_head(MU, Wmu)
        nc.sync.dma_start(out=eps_sb[:], in_=eps)

        ident = keep.tile([P, P], F32)
        make_identity(nc, ident[:])
        ident_bf = keep.tile([P, P], BF16)
        nc.vector.tensor_copy(out=ident_bf[:], in_=ident[:])
        kl_cols = keep.tile([P, 32], F32, align_bytes=64)
        nc.vector.memset(kl_cols[:], 0.0)
        half = keep.tile([P, 1], F32)
        nc.vector.memset(half[:], 0.5)

        def bank(name, index, shape, dtype=F32):
            return psum.tile(shape, dtype, name=name, tag="bank%d" % index)

        x_t = bank("x_t", 7, [P, G, 2, BATCH])
        acc = {}
        x_grouped = keep.tile([P, G * BATCH * PACK], BF16, align_bytes=64)
        x_codes = keep.tile([P, G, BATCH], U32, align_bytes=64)
        x_scales = keep.tile([P, G, BATCH], U8, align_bytes=64)
        w_grouped, w_codes, w_scales = {}, {}, {}
        h_plain, h_grouped, h_codes, h_scales = {}, {}, {}, {}
        head_grouped, head_codes, head_scales, sums = {}, {}, {}, {}
        for c in range(C):
            h_grouped[c] = keep.tile([P, BATCH, PACK], BF16, name="h_grouped%d" % c, align_bytes=64)
            h_codes[c] = keep.tile([P, BATCH], U32, name="h_codes%d" % c, align_bytes=64)
            h_scales[c] = keep.tile([P, BATCH], U8, name="h_scales%d" % c, align_bytes=64)
            h_plain[c] = keep.tile([P, PACK, BATCH], BF16, name="h_plain%d" % c)
            for g in range(G):
                for a in range(A):
                    tag = "%d%d%d" % (c, g, a)
                    w_grouped[(c, g, a)] = keep.tile([P, E, P, PACK], BF16, name="w_grouped" + tag, align_bytes=64)
                    w_codes[(c, g, a)] = keep.tile([P, E, P], U32, name="w_codes" + tag, align_bytes=64)
                    w_scales[(c, g, a)] = keep.tile([P, E, P], U8, name="w_scales" + tag, align_bytes=64)
        for head in (LS, MU):
            head_grouped[head] = keep.tile([P, C, LATENT, PACK], BF16, name="head_grouped%d" % head, align_bytes=64)
            head_codes[head] = keep.tile([P, C, LATENT], U32, name="head_codes%d" % head, align_bytes=64)
            head_scales[head] = keep.tile([P, C, LATENT], U8, name="head_scales%d" % head, align_bytes=64)

        def x_transposes():
            words = x_sb[:].bitcast(F32).rearrange("b (g p u) -> b g u p", g=G, u=2)
            for g in range(G):
                for u in range(2):
                    nc.tensor.transpose(out=x_t[:, g, u, :], in_=words[:, g, u, :], identity=ident[:])

        def x_copy():
            nc.scalar.copy(
                out=x_grouped[:].bitcast(F32).rearrange("p (g b u) -> p g b u", g=G, u=2),
                in_=x_t[:].rearrange("p g u b -> p g b u"),
            )

        def x_quantise():
            nc.vector.quantize_mx(
                out=x_codes[:].rearrange("p g b -> p (g b)").bitcast(FP8X4),
                scales=x_scales[:].rearrange("p g b -> p (g b)"),
                in_=x_grouped[:],
            )

        def w_copy(c, g, a):
            src = w_raw[(c, g, a)].rearrange("p j (n i) -> p n j i", i=4)
            dst = w_grouped[(c, g, a)][:].rearrange("p e (n i) j -> p (e n) j i", i=4)
            nc.vector.tensor_copy(out=dst[:, : V_COLS // 4], in_=src[:, : V_COLS // 4])
            nc.scalar.copy(out=dst[:, V_COLS // 4 :], in_=src[:, V_COLS // 4 :])

        def w_quantise(c, g, a):
            unit = (c, g, a)
            nc.vector.quantize_mx(
                out=w_codes[unit][:].rearrange("p e q -> p (e q)").bitcast(FP8X4),
                scales=w_scales[unit][:].rearrange("p e q -> p (e q)"),
                in_=w_grouped[unit][:].rearrange("p e q j -> p (e q j)"),
            )

        def tile_quantise(c, g, a, e):
            unit = (c, g, a)
            nc.vector.quantize_mx(
                out=w_codes[unit][:, e, :].bitcast(FP8X4),
                scales=w_scales[unit][:, e, :],
                in_=w_grouped[unit][:, e].rearrange("p q j -> p (q j)"),
            )

        def w_matmul(c, g, a, tiles=range(E)):
            for e in tiles:
                t = E * a + e
                if g == 0:
                    acc[(c, t)] = bank("acc%d%d" % (c, t), 4 * c + t, [P, BATCH])
                nc.tensor.matmul_mx(
                    out=acc[(c, t)][:],
                    lhsT=w_codes[(c, g, a)][:, e, :].bitcast(FP8X4),
                    lhsT_scale=w_scales[(c, g, a)][:, e, :],
                    rhs=x_codes[:, g, :].bitcast(FP8X4),
                    rhs_scale=x_scales[:, g, :],
                    start=(g == 0),
                    stop=(g == G - 1),
                )

        def relu_scalar(c, a, e):
            t = E * a + e
            nc.scalar.activation(
                out=h_plain[c][:, t, :], in_=acc[(c, t)][:], func=ACT.Relu, bias=be1_sb[:, c, t : t + 1]
            )

        def relu_vector(c, a, e):
            t = E * a + e
            nc.vector.tensor_scalar(
                out=h_plain[c][:, t, :],
                in0=acc[(c, t)][:],
                scalar1=be1_sb[:, c, t : t + 1],
                scalar2=0.0,
                op0=ALU.add,
                op1=ALU.max,
            )

        def h_copy(c):
            nc.vector.tensor_copy(
                out=h_grouped[c][:].rearrange("p (n i) t -> p n t i", i=4),
                in_=h_plain[c][:].rearrange("p t (n i) -> p n t i", i=4),
            )

        def h_quantise(c):
            nc.vector.quantize_mx(
                out=h_codes[c][:].bitcast(FP8X4),
                scales=h_scales[c][:],
                in_=h_grouped[c][:].rearrange("p b t -> p (b t)"),
            )

        def head_copy(copy, head, c, lo, hi):
            copy(
                out=head_grouped[head][:, c, lo:hi, :].rearrange("p (n i) t -> p n t i", i=4),
                in_=head_raw[head][:, c, :, lo:hi].rearrange("p t (n i) -> p n t i", i=4),
            )

        def head_quantise(head, c):
            nc.vector.quantize_mx(
                out=head_codes[head][:, c, :].bitcast(FP8X4),
                scales=head_scales[head][:, c, :],
                in_=head_grouped[head][:, c].rearrange("p l t -> p (l t)"),
            )

        def head_matmul(head, c):
            if c == 0:
                sums[head] = bank("sums%d" % head, head, [P, LATENT])
            nc.tensor.matmul_mx(
                out=sums[head][:],
                lhsT=h_codes[c][:].bitcast(FP8X4),
                lhsT_scale=h_scales[c][:],
                rhs=head_codes[head][:, c, :].bitcast(FP8X4),
                rhs_scale=head_scales[head][:, c, :],
                start=(c == 0),
                stop=(c == C - 1),
            )

        w_copy(0, 0, 0)
        w_copy(0, 0, 1)
        x_transposes()
        x_copy()
        w_quantise(0, 0, 0)
        w_quantise(0, 0, 1)
        w_copy(0, 1, 0)
        x_quantise()
        w_matmul(0, 0, 0)
        w_matmul(0, 0, 1)
        w_copy(0, 1, 1)
        w_quantise(0, 1, 0)
        w_matmul(0, 1, 0)
        w_quantise(0, 1, 1)
        w_matmul(0, 1, 1)
        be1_t = bank("be1_t", 7, [P, P], BF16)
        nc.tensor.transpose(out=be1_t[:], in_=rows[:], identity=ident_bf[:])
        head_copy(nc.vector.tensor_copy, LS, 0, 0, LATENT)
        head_copy(nc.scalar.copy, LS, 1, 0, LATENT)
        for a in range(A):
            w_copy(1, 0, a)
        for c in range(C):
            head_quantise(LS, c)
        nc.scalar.copy(out=be1_sb[:].rearrange("p c t -> p (c t)"), in_=be1_t[:, 0 : C * PACK])
        for a in range(A):
            w_quantise(1, 0, a)
            w_matmul(1, 0, a)
        for a in range(A):
            for e in range(E):
                relu_scalar(0, a, e)
        for a in range(A):
            w_copy(1, 1, a)
        w_quantise(1, 1, 0)
        w_matmul(1, 1, 0)
        for e in range(E):
            tile_quantise(1, 1, 1, e)
            w_matmul(1, 1, 1, (e,))
        head_bias_ps = bank("head_bias_ps", 2, [P, 2, LATENT], BF16)
        for head in (MU, LS):
            for r in range(BIAS_ROWS):
                row = first_bias_row[head] + r
                width = LATENT // BIAS_ROWS
                nc.tensor.matmul(
                    out=head_bias_ps[:, head, r * width : (r + 1) * width],
                    lhsT=ident_bf[:, row : row + 1].to_broadcast([P, P]),
                    rhs=rows[:, 0:width],
                    start=True,
                    stop=True,
                )
        h_copy(0)
        head_copy(nc.scalar.copy, MU, 0, 0, LATENT)
        relu_scalar(1, 0, 0)
        relu_scalar(1, 0, 1)
        head_quantise(MU, 0)
        relu_scalar(1, 1, 0)
        relu_vector(1, 1, 1)
        h_quantise(0)
        head_matmul(LS, 0)
        head_matmul(MU, 0)
        head_bias = keep.tile([P, 2, LATENT], BF16)
        nc.scalar.copy(out=head_bias[:], in_=head_bias_ps[:])
        head_copy(nc.scalar.copy, MU, 1, 0, LATENT)
        h_copy(1)
        h_quantise(1)
        head_matmul(LS, 1)
        head_quantise(MU, 1)
        head_matmul(MU, 1)

        log_sigma = keep.tile([P, LATENT], F32)
        nc.vector.tensor_tensor(out=log_sigma[:], in0=sums[LS][:], in1=head_bias[:, LS, :], op=ALU.add)
        mu = keep.tile([P, LATENT], F32)
        nc.vector.tensor_tensor(out=mu[:], in0=sums[MU][:], in1=head_bias[:, MU, :], op=ALU.add)
        sigma = keep.tile([P, LATENT], F32)
        nc.scalar.activation(out=sigma[:], in_=log_sigma[:], func=ACT.Exp)
        noise = keep.tile([P, LATENT], F32)
        nc.vector.tensor_tensor(out=noise[:], in0=sigma[:], in1=eps_sb[:], op=ALU.mult)
        terms = keep.tile([P, 3, LATENT], F32)
        kl_sums = keep.tile([P, 3], F32)
        for i, (values, func, scale, bias) in enumerate(
            (
                (sigma, ACT.Square, 0.5**0.5, 0.0),
                (log_sigma, ACT.Identity, 1.0, half[:]),
                (mu, ACT.Square, 0.5**0.5, 0.0),
            )
        ):
            nc.scalar.activation(
                out=terms[:, i, :],
                in_=values[:],
                func=func,
                scale=scale,
                bias=bias,
                accum_out=kl_sums[:, i : i + 1],
            )
        z = keep.tile([P, LATENT], F32)
        nc.vector.tensor_tensor(out=z[:], in0=noise[:], in1=mu[:], op=ALU.add)
        nc.sync.dma_start(out=out_0, in_=z[:])
        nc.vector.tensor_scalar(
            out=kl_cols[:, 0:1],
            in0=kl_sums[:, 0:1],
            scalar1=kl_sums[:, 2:3],
            scalar2=kl_sums[:, 1:2],
            op0=ALU.add,
            op1=ALU.subtract,
        )
        kl_rows = keep.tile([P, 32], F32, align_bytes=64)
        nc.vector.transpose(kl_rows[:], kl_cols[:])
        nc.scalar.dma_start(out=out_1.rearrange("(a b) -> a b", b=32), in_=kl_rows[0:P:32, :])
